import numpy as np
import ml_dtypes


def mxq(x, axis, fmt="e4m3"):
    dtype, down = {"e4m3": (ml_dtypes.float8_e4m3fn, 7), "e5m2": (ml_dtypes.float8_e5m2, 14)}[fmt]
    v = np.moveaxis(np.asarray(x, np.float32).astype(ml_dtypes.bfloat16).astype(np.float64), axis, -1)
    blocks = v.reshape(v.shape[:-1] + (-1, 32))
    amax = np.abs(blocks).max(-1, keepdims=True)
    byte = np.maximum(np.where(amax > 0, np.frexp(amax)[1] - 1 + 127, 0) - down, 1)
    scale = np.exp2(byte - 127.0)
    codes = (blocks / scale).astype(np.float32).astype(dtype).astype(np.float64)
    return np.moveaxis((codes * scale).reshape(v.shape), -1, axis)


WIDE = False


def mx_kscale(k):
    if not WIDE:
        return np.ones(k)
    levels = np.array([10, -10, 5, -5, 0])
    a = np.random.permutation(np.resize(levels, k // 512 * 4)).reshape(k // 512, 4)
    idx = np.arange(k)
    return np.exp2(a[idx // 512, idx % 128 // 32])


BF16 = ml_dtypes.bfloat16


def bf(x):
    return np.asarray(x, np.float32).astype(BF16)


def f64(x):
    return np.asarray(x).astype(np.float64)


E2M1 = np.array([0.0, 0.5, 1.0, 1.5, 2.0, 3.0, 4.0, 6.0, -0.0, -0.5, -1.0, -1.5, -2.0, -3.0, -4.0, -6.0])


def pack_weight(w, fmt):
    k, n = w.shape
    w = f64(bf(w)).reshape(k // 32, 32, n)
    amax = np.abs(w).max(1)
    if fmt == "e4m3":
        byte = np.frexp(amax)[1] - 1 + 127 - 7
    else:
        mant, ex = np.frexp(amax / 6.0)
        byte = np.where(mant > 0.5, ex, ex - 1) + 127
    byte = np.clip(np.where(amax > 0, byte, 1), 1, 254)
    scaled = (w * np.exp2(127.0 - byte)[:, None, :]).reshape(k, n).astype(np.float32)
    by_word = np.ascontiguousarray(scaled.reshape(k // 512, 128, 4, n).transpose(0, 1, 3, 2))
    if fmt == "e4m3":
        words = by_word.astype(ml_dtypes.float8_e4m3fn).view(np.uint8)
    else:
        c = by_word.astype(ml_dtypes.float4_e2m1fn).view(np.uint8) & 0xF
        words = c[..., 0::2] | (c[..., 1::2] << 4)
    return np.ascontiguousarray(words), np.ascontiguousarray(byte.astype(np.uint8).reshape(k // 512, 16, n))


def unpack_weight(words, scales, fmt):
    g, p, n, _ = words.shape
    if fmt == "e4m3":
        vals = np.ascontiguousarray(words).view(ml_dtypes.float8_e4m3fn).astype(np.float64)
    else:
        nib = np.empty((g, p, n, 4), np.uint8)
        nib[..., 0::2] = words & 0xF
        nib[..., 1::2] = words >> 4
        vals = E2M1[nib]
    vals = vals * np.repeat(np.exp2(scales.astype(np.float64) - 127.0), 8, axis=1)[..., None]
    return vals.transpose(0, 1, 3, 2).reshape(g * 512, n)

def pack4(w):
    words, scales = pack_weight(w, "e2m1")
    return words.reshape(words.shape[0], 128, -1), scales


def unpack4(words, scales):
    return unpack_weight(words.reshape(words.shape[0], 128, -1, 2), scales, "e2m1")


B, H = 512, 1024
EPS = 1e-5


def layernorm(x, gamma, beta):
    mu = np.mean(x, axis=-1, keepdims=True)
    var = np.var(x, axis=-1, keepdims=True)
    return (x - mu) / np.sqrt(var + EPS) * gamma + beta


def sigmoid(v):
    return 1.0 / (1.0 + np.exp(-v))


def setup_inputs():
    s = mx_kscale(H)
    inp = bf(np.random.standard_normal((B, H)) * s)
    hx = bf(np.random.standard_normal((B, H)))
    W_words, W_scales = pack4(np.random.standard_normal((H, 3 * H)) / np.sqrt(H) / s[:, None])
    U_words, U_scales = pack4(np.random.standard_normal((H, 3 * H)) / np.sqrt(H))
    return {"input": inp,
            "hx": hx,
            "W_words": W_words,
            "W_scales": W_scales,
            "U_words": U_words,
            "U_scales": U_scales,
            "b": bf(np.random.standard_normal(3 * H) * 0.1),
            "W_gamma": bf(1.0 + np.random.standard_normal(3 * H) * 0.1),
            "W_beta": bf(np.random.standard_normal(3 * H) * 0.1),
            "U_gamma": bf(1.0 + np.random.standard_normal(3 * H) * 0.1),
            "U_beta": bf(np.random.standard_normal(3 * H) * 0.1)}


def reference(input, hx, W_words, W_scales, U_words, U_scales, b, W_gamma, W_beta, U_gamma, U_beta):
    hx = f64(hx)
    b = f64(b)
    xw = layernorm(mxq(f64(input), 1, "e4m3") @ unpack4(W_words, W_scales), f64(W_gamma), f64(W_beta))
    hu = layernorm(mxq(hx, 1, "e4m3") @ unpack4(U_words, U_scales), f64(U_gamma), f64(U_beta))
    xw0, xw1, xw2 = xw[:, :H], xw[:, H:2 * H], xw[:, 2 * H:]
    hu0, hu1, hu2 = hu[:, :H], hu[:, H:2 * H], hu[:, 2 * H:]
    b0, b1, b2 = b[:H], b[H:2 * H], b[2 * H:]
    z = sigmoid(xw0 + hu0 + b0)
    r = sigmoid(xw1 + hu1 + b1)
    hx_ = np.tanh(r * hu2 + xw2 + b2)
    return (1.0 - z) * hx_ + z * hx

@@ -1,0 +1,281 @@
+from contextlib import ExitStack
+
+import concourse.mybir as mybir
+from concourse.masks import make_identity
+
+F32 = mybir.dt.float32
+BF16 = mybir.dt.bfloat16
+U8 = mybir.dt.uint8
+U32 = mybir.dt.uint32
+I32 = mybir.dt.int32
+FP8X4 = mybir.dt.float8_e4m3fn_x4
+FP4X4 = mybir.dt.float4_e2m1fn_x4
+ALU = mybir.AluOpType
+ACT = mybir.ActivationFunctionType
+AX = mybir.AxisListType
+
+P = 128
+B = 512
+H = 1024
+N3 = 3 * H
+NB = 512
+BANKS = N3 // NB
+G = H // 512
+BT = B // P
+EPS = 1e-5
+FLOPS = 2 * 2 * B * H * N3
+
+
+def tile_lngrucell_kernel(tc, x_in, hx, W_words, W_scales, U_words, U_scales,
+                                      b, W_gamma, W_beta, U_gamma, U_beta, out):
+    nc = tc.nc
+    with ExitStack() as ctx:
+        const = ctx.enter_context(tc.tile_pool(name="const", bufs=1))
+        xin = ctx.enter_context(tc.tile_pool(name="xin", bufs=2))
+        work = ctx.enter_context(tc.tile_pool(name="work", bufs=3))
+        small = ctx.enter_context(tc.tile_pool(name="small", bufs=4))
+        psum = ctx.enter_context(tc.psum_pool(name="psum", bufs=1))
+        ctx.enter_context(tc.manual_schedule())
+
+        planes = [const.tile([P, G, N3], U8, name="plane%d" % w, align_bytes=64) for w in range(2)]
+        words = [const.tile([P, G, 2 * N3], U8, name="words%d" % w, align_bytes=64) for w in range(2)]
+        vecs = const.tile([P, N3], BF16, name="vecs")
+        mhalf = const.tile([P, 1], F32, name="mhalf")
+        warm = const.tile([P, 1], F32, name="warm")
+        ident = const.tile([P, P], F32, name="ident")
+        make_identity(nc, ident[:])
+        nc.vector.memset(vecs[:].bitcast(I32), 0)
+        nc.vector.memset(planes[0][:].rearrange("p g n -> p (g n)").bitcast(I32), 0)
+        nc.vector.memset(planes[1][:].rearrange("p g n -> p (g n)").bitcast(I32), 0)
+        nc.vector.memset(mhalf[:], -0.5)
+
+        for r, v in enumerate((W_gamma, U_gamma, U_beta, W_beta, b)):
+            nc.scalar.dma_start(out=vecs[r:r + 1, :], in_=v.rearrange("(o n) -> o n", o=1))
+        nc.scalar.activation(out=warm[:], in_=mhalf[:], func=ACT.Sigmoid)
+
+        x_sb = [const.tile([P, H], BF16, name="x_sb%d" % i) for i in range(BT)]
+        h_sb = [const.tile([P, H], BF16, name="h_sb%d" % i) for i in range(BT)]
+
+        def load_rows(dst, src, i):
+            nc.sync.dma_start(out=dst[i][:], in_=src[i * P:(i + 1) * P, :])
+
+        def load_scales(w, src):
+            for half in range(2):
+                for r in range(4):
+                    p0 = 32 * half + r
+                    q0 = 4 * half + r
+                    nc.sync.dma_start(
+                        out=planes[w][p0:P:64, :, :].bitcast(I32),
+                        in_=src[:, q0:16:8, :].rearrange("g q n -> q g n").bitcast(I32),
+                    )
+
+        def load_words(w, src):
+            step = 2 * N3 // 3
+            for c in range(3):
+                nc.sync.dma_start(
+                    out=words[w][:, :, c * step:(c + 1) * step].bitcast(I32),
+                    in_=src[:, :, c * step:(c + 1) * step].rearrange("g p c -> p g c").bitcast(I32),
+                )
+
+        load_rows(x_sb, x_in, 0)
+        load_rows(h_sb, hx, 0)
+        load_scales(0, W_scales)
+        load_words(0, W_words)
+        load_scales(1, U_scales)
+        load_words(1, U_words)
+        for i in range(1, BT):
+            load_rows(x_sb, x_in, i)
+            load_rows(h_sb, hx, i)
+
+        coef32 = const.tile([P, 8], F32, name="coef32")
+        coefb = const.tile([P, 8], BF16, name="coefb")
+        nc.vector.tensor_copy(out=coef32[:, 0:3], in_=ident[:, 0:3])
+        nc.vector.tensor_reduce(out=coef32[:, 3:4], in_=ident[:, 2:5], axis=AX.X, op=ALU.add)
+        nc.vector.tensor_reduce(out=coef32[:, 4:5], in_=ident[:, 3:5], axis=AX.X, op=ALU.add)
+        nc.vector.tensor_copy(out=coefb[:, 0:5], in_=coef32[:, 0:5])
+
+        gam = [const.tile([P, N3], F32, name="gam%d" % w) for w in range(2)]
+        B01 = const.tile([P, 2 * H], F32, name="B01")
+        B2 = const.tile([P, H], F32, name="B2")
+        bU2 = const.tile([P, H], F32, name="bU2")
+
+        spread_count = [0]
+
+        def spread(dst, c, j0, nj):
+            for j in range(nj):
+                ps = psum.tile([P, NB], F32, name="ps", tag="acc", bufs=6)
+                nc.tensor.matmul(out=ps[:], lhsT=coefb[:, c:c + 1].to_broadcast([P, P]),
+                                 rhs=vecs[:, (j0 + j) * NB:(j0 + j + 1) * NB], start=True, stop=True)
+                if spread_count[0] % 2 == 0:
+                    nc.scalar.copy(out=dst[:, j * NB:(j + 1) * NB], in_=ps[:])
+                else:
+                    nc.vector.tensor_copy(out=dst[:, j * NB:(j + 1) * NB], in_=ps[:])
+                spread_count[0] += 1
+
+        codes = {}
+        scls = {}
+
+        def prep(i, w):
+            src32 = (x_sb[i] if w == 0 else h_sb[i])[:].bitcast(F32)
+            xt = psum.tile([P, NB], F32, name="xt", tag="xt", bufs=1)
+            for g in range(G):
+                for u in range(2):
+                    nc.tensor.transpose(xt[:, (2 * g + u) * P:(2 * g + u + 1) * P],
+                                        src32[:, 256 * g + u:256 * (g + 1):2], ident[:])
+            grouped = xin.tile([P, NB], F32, name="grouped", tag="grouped", align_bytes=64)
+            nc.scalar.copy(
+                out=grouped[:].rearrange("p (g b u) -> p g b u", g=G, u=2),
+                in_=xt[:].rearrange("p (g u b) -> p g b u", g=G, u=2),
+            )
+            cd = const.tile([P, G * P], U32, name="codes%d_%d" % (w, i), align_bytes=64)
+            sc = const.tile([P, G * P], U8, name="scl%d_%d" % (w, i), align_bytes=64)
+            nc.vector.quantize_mx(out=cd[:].bitcast(FP8X4), scales=sc[:], in_=grouped[:].bitcast(BF16))
+            codes[(i, w)] = cd
+            scls[(i, w)] = sc
+
+        def mx(dst, i, w, j, g, start, stop):
+            nc.tensor.matmul_mx(
+                out=dst[:],
+                lhsT=codes[(i, w)][:, g * P:(g + 1) * P].bitcast(FP8X4),
+                lhsT_scale=scls[(i, w)][:, g * P:(g + 1) * P],
+                rhs=words[w][:, g, 2 * NB * j:2 * NB * (j + 1)].bitcast(FP4X4),
+                rhs_scale=planes[w][:, g, NB * j:NB * (j + 1)],
+                start=start, stop=stop,
+            )
+
+        folds = {}
+        mus = {}
+        s2s = {}
+        rss = {}
+
+        def fold(i, w):
+            f = psum.tile([P, NB], F32, name="fold", tag="fold", bufs=1)
+            for j in range(BANKS):
+                for g in range(G):
+                    mx(f, i, w, j, g, j == 0 and g == 0, j == BANKS - 1 and g == G - 1)
+            folds[(i, w)] = f
+
+        def mean(i, w):
+            mu = small.tile([P, 1], F32, name="mu", tag="mu")
+            junk = small.tile([P, NB], BF16, name="junk", tag="junk")
+            nc.scalar.activation(out=junk[:], in_=folds[(i, w)][:], func=ACT.Identity, scale=1.0 / N3,
+                                 accum_out=mu[:])
+            mus[(i, w)] = mu
+
+        def unit(i, w, dst):
+            mu = mus[(i, w)]
+            s2 = small.tile([P, BANKS], F32, name="s2", tag="s2")
+            for j in range(BANKS):
+                acc = psum.tile([P, NB], F32, name="acc", tag="acc", bufs=6)
+                for g in range(G):
+                    mx(acc, i, w, j, g, g == 0, g == G - 1)
+                junk = small.tile([P, NB], BF16, name="junk", tag="junk")
+                nc.scalar.activation(out=junk[:], in_=acc[:], func=ACT.Square, scale=-1.0, bias=mu[:, 0:1],
+                                     accum_out=s2[:, j:j + 1])
+                nc.vector.scalar_tensor_tensor(out=dst[:, j * NB:(j + 1) * NB], in0=acc[:], scalar=mu[:, 0:1],
+                                               in1=gam[w][:, j * NB:(j + 1) * NB], op0=ALU.subtract, op1=ALU.mult)
+            vs = small.tile([P, 1], F32, name="vs", tag="vs")
+            rs = small.tile([P, 1], F32, name="rs", tag="rs")
+            nc.vector.tensor_reduce(out=vs[:], in_=s2[:], axis=AX.X, op=ALU.add)
+            nc.gpsimd.tensor_scalar(out=vs[:], in0=vs[:], scalar1=1.0 / N3, scalar2=EPS, op0=ALU.mult, op1=ALU.add)
+            nc.gpsimd.tensor_tensor(out=rs[:], in0=vs[:], in1=mhalf[:], op=ALU.pow)
+            rss[(i, w)] = rs
+
+        us = {}
+        ws = {}
+
+        def cols(part, lo, hi):
+            return slice(part * H + lo, part * H + hi)
+
+        def scale_a(i, part, lo=0, hi=H):
+            bias = B2[:, lo:hi] if part == 2 else B01[:, cols(part, lo, hi)]
+            u = us[i][:, cols(part, lo, hi)]
+            nc.vector.scalar_tensor_tensor(out=u, in0=u, scalar=rss[(i, 0)][:, 0:1], in1=bias,
+                                           op0=ALU.mult, op1=ALU.add)
+
+        def add_c(i, part, lo=0, hi=H):
+            u = us[i][:, cols(part, lo, hi)]
+            nc.vector.scalar_tensor_tensor(out=u, in0=ws[i][:, cols(part, lo, hi)], scalar=rss[(i, 1)][:, 0:1], in1=u,
+                                           op0=ALU.mult, op1=ALU.add)
+
+        def hu2(i, lo=0, hi=H):
+            t = ws[i][:, cols(2, lo, hi)]
+            nc.vector.scalar_tensor_tensor(out=t, in0=t, scalar=rss[(i, 1)][:, 0:1], in1=bU2[:, lo:hi],
+                                           op0=ALU.mult, op1=ALU.add)
+
+        def gate(i, part, lo=0, hi=H):
+            u = us[i][:, cols(part, lo, hi)]
+            nc.scalar.activation(out=u, in_=u, func=ACT.Tanh if part == 2 else ACT.Sigmoid)
+
+        def cand(eng, i, lo=0, hi=H):
+            t = ws[i][:, cols(2, lo, hi)]
+            n = us[i][:, cols(2, lo, hi)]
+            eng.tensor_tensor(out=t, in0=us[i][:, cols(1, lo, hi)], in1=t, op=ALU.mult)
+            eng.tensor_tensor(out=n, in0=t, in1=n, op=ALU.add)
+
+        def blend(eng, i, lo=0, hi=H):
+            t = ws[i][:, cols(2, lo, hi)]
+            n = us[i][:, cols(2, lo, hi)]
+            eng.tensor_tensor(out=t, in0=h_sb[i][:, lo:hi], in1=n, op=ALU.subtract)
+            eng.tensor_tensor(out=t, in0=us[i][:, cols(0, lo, hi)], in1=t, op=ALU.mult)
+            eng.tensor_tensor(out=t, in0=t, in1=n, op=ALU.add)
+            nc.sync.dma_start(out=out[i * P:(i + 1) * P, lo:hi], in_=t)
+
+        spread(gam[0], 0, 0, BANKS)
+        prep(0, 0)
+        prep(0, 1)
+        fold(0, 0)
+        mean(0, 0)
+        for i in range(BT):
+            us[i] = work.tile([P, N3], F32, name="u", tag="u")
+            ws[i] = work.tile([P, N3], F32, name="wt", tag="wt")
+            unit(i, 0, us[i])
+            if i == 0:
+                spread(B01, 3, 0, 4)
+                spread(B2, 4, 4, 2)
+                spread(gam[1], 1, 0, BANKS)
+            if i + 1 < BT:
+                prep(i + 1, 0)
+            fold(i, 1)
+            if i > 0:
+                gate(i - 1, 1)
+                gate(i - 1, 0)
+            mean(i, 1)
+            if i > 0:
+                cand(nc.gpsimd, i - 1)
+            if i == 0:
+                scale_a(i, 1)
+                scale_a(i, 2)
+                scale_a(i, 0)
+            unit(i, 1, ws[i])
+            if i == 0:
+                spread(bU2, 2, 4, 2)
+            if i + 1 < BT:
+                prep(i + 1, 1)
+                fold(i + 1, 0)
+            if i > 0:
+                gate(i - 1, 2)
+                blend(nc.gpsimd, i - 1)
+            if i + 1 < BT:
+                mean(i + 1, 0)
+            if i > 0:
+                scale_a(i, 1)
+                scale_a(i, 2)
+                scale_a(i, 0)
+            if i + 1 < BT:
+                add_c(i, 1)
+                hu2(i)
+                add_c(i, 0)
+        last = BT - 1
+        halves = ((0, H // 2), (H // 2, H))
+        for lo, hi in halves:
+            add_c(last, 1, lo, hi)
+            hu2(last, lo, hi)
+            gate(last, 1, lo, hi)
+        for lo, hi in halves:
+            add_c(last, 0, lo, hi)
+            gate(last, 0, lo, hi)
+            cand(nc.vector, last, lo, hi)
+            gate(last, 2, lo, hi)
+        for lo, hi in halves:
+            blend(nc.vector, last, lo, hi)

@@ -101,12 +101,12 @@ def tile_lngrucell_kernel(tc, x_in, hx, W_words, W_scales, U_words, U_scales,
 
         spread_count = [0]
 
-        def spread(dst, c, j0, nj):
+        def spread(dst, c, j0, nj, both=True):
             for j in range(nj):
                 ps = psum.tile([P, NB], F32, name="ps", tag="acc", bufs=6)
                 nc.tensor.matmul(out=ps[:], lhsT=coefb[:, c:c + 1].to_broadcast([P, P]),
                                  rhs=vecs[:, (j0 + j) * NB:(j0 + j + 1) * NB], start=True, stop=True)
-                if spread_count[0] % 2 == 0:
+                if spread_count[0] % 2 == 0 or not both:
                     nc.scalar.copy(out=dst[:, j * NB:(j + 1) * NB], in_=ps[:])
                 else:
                     nc.vector.tensor_copy(out=dst[:, j * NB:(j + 1) * NB], in_=ps[:])
@@ -115,7 +115,9 @@ def tile_lngrucell_kernel(tc, x_in, hx, W_words, W_scales, U_words, U_scales,
         codes = {}
         scls = {}
 
-        def prep(i, w):
+        groups = {}
+
+        def prep_t(i, w):
             src32 = (x_sb[i] if w == 0 else h_sb[i])[:].bitcast(F32)
             xt = psum.tile([P, NB], F32, name="xt", tag="xt", bufs=1)
             for g in range(G):
@@ -127,6 +129,10 @@ def tile_lngrucell_kernel(tc, x_in, hx, W_words, W_scales, U_words, U_scales,
                 out=grouped[:].rearrange("p (g b u) -> p g b u", g=G, u=2),
                 in_=xt[:].rearrange("p (g u b) -> p g b u", g=G, u=2),
             )
+            groups[(i, w)] = grouped
+
+        def prep_q(i, w):
+            grouped = groups[(i, w)]
             cd = const.tile([P, G * P], U32, name="codes%d_%d" % (w, i), align_bytes=64)
             sc = const.tile([P, G * P], U8, name="scl%d_%d" % (w, i), align_bytes=64)
             nc.vector.quantize_mx(out=cd[:].bitcast(FP8X4), scales=sc[:], in_=grouped[:].bitcast(BF16))
@@ -176,8 +182,9 @@ def tile_lngrucell_kernel(tc, x_in, hx, W_words, W_scales, U_words, U_scales,
                                                in1=gam[w][:, j * NB:(j + 1) * NB], op0=ALU.subtract, op1=ALU.mult)
             vs = small.tile([P, 1], F32, name="vs", tag="vs")
             rs = small.tile([P, 1], F32, name="rs", tag="rs")
-            nc.vector.tensor_reduce(out=vs[:], in_=s2[:], axis=AX.X, op=ALU.add)
-            nc.gpsimd.tensor_scalar(out=vs[:], in0=vs[:], scalar1=1.0 / N3, scalar2=EPS, op0=ALU.mult, op1=ALU.add)
+            j6 = small.tile([P, BANKS], F32, name="j6", tag="j6")
+            nc.scalar.activation(out=j6[:], in_=s2[:], func=ACT.Identity, scale=1.0 / N3, bias=EPS / BANKS,
+                                 accum_out=vs[:])
             nc.gpsimd.tensor_tensor(out=rs[:], in0=vs[:], in1=mhalf[:], op=ALU.pow)
             rss[(i, w)] = rs
 
@@ -213,17 +220,27 @@ def tile_lngrucell_kernel(tc, x_in, hx, W_words, W_scales, U_words, U_scales,
             eng.tensor_tensor(out=t, in0=us[i][:, cols(1, lo, hi)], in1=t, op=ALU.mult)
             eng.tensor_tensor(out=n, in0=t, in1=n, op=ALU.add)
 
-        def blend(eng, i, lo=0, hi=H):
+        def blend_d(eng, i, lo=0, hi=H):
+            eng.tensor_tensor(out=ws[i][:, cols(2, lo, hi)], in0=h_sb[i][:, lo:hi], in1=us[i][:, cols(2, lo, hi)],
+                              op=ALU.subtract)
+
+        def blend_e(eng, i, lo=0, hi=H):
             t = ws[i][:, cols(2, lo, hi)]
-            n = us[i][:, cols(2, lo, hi)]
-            eng.tensor_tensor(out=t, in0=h_sb[i][:, lo:hi], in1=n, op=ALU.subtract)
             eng.tensor_tensor(out=t, in0=us[i][:, cols(0, lo, hi)], in1=t, op=ALU.mult)
-            eng.tensor_tensor(out=t, in0=t, in1=n, op=ALU.add)
+
+        def blend_o(eng, i, lo=0, hi=H):
+            t = ws[i][:, cols(2, lo, hi)]
+            eng.tensor_tensor(out=t, in0=t, in1=us[i][:, cols(2, lo, hi)], op=ALU.add)
             nc.sync.dma_start(out=out[i * P:(i + 1) * P, lo:hi], in_=t)
 
+        halves = ((0, H // 2), (H // 2, H))
         spread(gam[0], 0, 0, BANKS)
-        prep(0, 0)
-        prep(0, 1)
+        prep_t(0, 0)
+        prep_q(0, 0)
+        spread(B01, 3, 0, 4)
+        spread(B2, 4, 4, 2)
+        prep_t(0, 1)
+        prep_q(0, 1)
         fold(0, 0)
         mean(0, 0)
         for i in range(BT):
@@ -231,51 +248,49 @@ def tile_lngrucell_kernel(tc, x_in, hx, W_words, W_scales, U_words, U_scales,
             ws[i] = work.tile([P, N3], F32, name="wt", tag="wt")
             unit(i, 0, us[i])
             if i == 0:
-                spread(B01, 3, 0, 4)
-                spread(B2, 4, 4, 2)
                 spread(gam[1], 1, 0, BANKS)
             if i + 1 < BT:
-                prep(i + 1, 0)
+                prep_t(i + 1, 0)
             fold(i, 1)
             if i > 0:
-                gate(i - 1, 1)
                 gate(i - 1, 0)
+                for lo, hi in halves:
+                    gate(i - 1, 2, lo, hi)
+                for lo, hi in halves:
+                    blend_d(nc.gpsimd, i - 1, lo, hi)
+                for lo, hi in halves:
+                    blend_e(nc.gpsimd, i - 1, lo, hi)
             mean(i, 1)
-            if i > 0:
-                cand(nc.gpsimd, i - 1)
             if i == 0:
                 scale_a(i, 1)
                 scale_a(i, 2)
                 scale_a(i, 0)
+            if i + 1 < BT:
+                prep_q(i + 1, 0)
             unit(i, 1, ws[i])
             if i == 0:
-                spread(bU2, 2, 4, 2)
+                spread(bU2, 2, 4, 2, both=False)
             if i + 1 < BT:
-                prep(i + 1, 1)
+                prep_t(i + 1, 1)
+                prep_q(i + 1, 1)
                 fold(i + 1, 0)
-            if i > 0:
-                gate(i - 1, 2)
-                blend(nc.gpsimd, i - 1)
-            if i + 1 < BT:
                 mean(i + 1, 0)
             if i > 0:
+                blend_o(nc.vector, i - 1)
                 scale_a(i, 1)
                 scale_a(i, 2)
+            add_c(i, 1)
+            gate(i, 1)
+            hu2(i)
+            if i > 0:
                 scale_a(i, 0)
-            if i + 1 < BT:
-                add_c(i, 1)
-                hu2(i)
-                add_c(i, 0)
+            add_c(i, 0)
+            cand(nc.vector, i)
         last = BT - 1
-        halves = ((0, H // 2), (H // 2, H))
+        gate(last, 0)
         for lo, hi in halves:
-            add_c(last, 1, lo, hi)
-            hu2(last, lo, hi)
-            gate(last, 1, lo, hi)
-        for lo, hi in halves:
-            add_c(last, 0, lo, hi)
-            gate(last, 0, lo, hi)
-            cand(nc.vector, last, lo, hi)
             gate(last, 2, lo, hi)
         for lo, hi in halves:
-            blend(nc.vector, last, lo, hi)
+            blend_d(nc.vector, last, lo, hi)
+            blend_e(nc.vector, last, lo, hi)
+            blend_o(nc.vector, last, lo, hi)

@@ -24,6 +24,7 @@ G = H // 512
 BT = B // P
 EPS = 1e-5
 FLOPS = 2 * 2 * B * H * N3
+HALVES = ((0, NB), (NB, H))
 
 
 def tile_lngrucell_kernel(tc, x_in, hx, W_words, W_scales, U_words, U_scales,
@@ -39,87 +40,94 @@ def tile_lngrucell_kernel(tc, x_in, hx, W_words, W_scales, U_words, U_scales,
 
         planes = [const.tile([P, G, N3], U8, name="plane%d" % w, align_bytes=64) for w in range(2)]
         words = [const.tile([P, G, 2 * N3], U8, name="words%d" % w, align_bytes=64) for w in range(2)]
-        vecs = const.tile([P, N3], BF16, name="vecs")
+        gvec = const.tile([P, N3], BF16, name="gvec")
+        bvec = const.tile([P, N3], BF16, name="bvec")
         mhalf = const.tile([P, 1], F32, name="mhalf")
         warm = const.tile([P, 1], F32, name="warm")
         ident = const.tile([P, P], F32, name="ident")
-        make_identity(nc, ident[:])
-        nc.vector.memset(vecs[:].bitcast(I32), 0)
-        nc.vector.memset(planes[0][:].rearrange("p g n -> p (g n)").bitcast(I32), 0)
-        nc.vector.memset(planes[1][:].rearrange("p g n -> p (g n)").bitcast(I32), 0)
-        nc.vector.memset(mhalf[:], -0.5)
-
-        for r, v in enumerate((W_gamma, U_gamma, U_beta, W_beta, b)):
-            nc.scalar.dma_start(out=vecs[r:r + 1, :], in_=v.rearrange("(o n) -> o n", o=1))
-        nc.scalar.activation(out=warm[:], in_=mhalf[:], func=ACT.Sigmoid)
-
         x_sb = [const.tile([P, H], BF16, name="x_sb%d" % i) for i in range(BT)]
         h_sb = [const.tile([P, H], BF16, name="h_sb%d" % i) for i in range(BT)]
+
+        make_identity(nc, ident[:])
+        nc.vector.memset(mhalf[:], -0.5)
+        nc.vector.memset(gvec[:].bitcast(I32), 0)
+        nc.vector.memset(planes[0][:].rearrange("p g n -> p (g n)").bitcast(I32), 0)
+        nc.vector.memset(planes[1][:].rearrange("p g n -> p (g n)").bitcast(I32), 0)
+        nc.vector.memset(bvec[:].bitcast(I32), 0)
 
         def load_rows(dst, src, i):
             nc.sync.dma_start(out=dst[i][:], in_=src[i * P:(i + 1) * P, :])
 
         def load_scales(w, src):
-            for half in range(2):
-                for r in range(4):
-                    p0 = 32 * half + r
-                    q0 = 4 * half + r
-                    nc.sync.dma_start(
-                        out=planes[w][p0:P:64, :, :].bitcast(I32),
-                        in_=src[:, q0:16:8, :].rearrange("g q n -> q g n").bitcast(I32),
-                    )
+            for r in range(4):
+                nc.sync.dma_start(
+                    out=planes[w][r:P:32, :, :].bitcast(I32),
+                    in_=src[:, r:16:4, :].rearrange("g q n -> q g n").bitcast(I32),
+                )
 
-        def load_words(w, src):
-            step = 2 * N3 // 3
-            for c in range(3):
+        def load_words(w, src, chunks):
+            step = 2 * N3 // chunks
+            for c in range(chunks):
                 nc.sync.dma_start(
                     out=words[w][:, :, c * step:(c + 1) * step].bitcast(I32),
                     in_=src[:, :, c * step:(c + 1) * step].rearrange("g p c -> p g c").bitcast(I32),
                 )
 
+        def load_vec(eng, dst, r, v):
+            eng.dma_start(out=dst[r:r + 1, :], in_=v.rearrange("(o n) -> o n", o=1))
+
         load_rows(x_sb, x_in, 0)
         load_rows(h_sb, hx, 0)
+        load_vec(nc.scalar, gvec, 0, W_gamma)
+        load_vec(nc.scalar, gvec, 1, U_gamma)
+        nc.scalar.activation(out=warm[:], in_=mhalf[:], func=ACT.Sigmoid)
         load_scales(0, W_scales)
-        load_words(0, W_words)
+        load_words(0, W_words, 2)
         load_scales(1, U_scales)
-        load_words(1, U_words)
-        for i in range(1, BT):
+        load_words(1, U_words, 2)
+        load_rows(x_sb, x_in, 1)
+        load_rows(h_sb, hx, 1)
+        for r, v in enumerate((U_beta, W_beta, b)):
+            load_vec(nc.sync, bvec, r, v)
+        for i in range(2, BT):
             load_rows(x_sb, x_in, i)
             load_rows(h_sb, hx, i)
 
-        coef32 = const.tile([P, 8], F32, name="coef32")
-        coefb = const.tile([P, 8], BF16, name="coefb")
-        nc.vector.tensor_copy(out=coef32[:, 0:3], in_=ident[:, 0:3])
-        nc.vector.tensor_reduce(out=coef32[:, 3:4], in_=ident[:, 2:5], axis=AX.X, op=ALU.add)
-        nc.vector.tensor_reduce(out=coef32[:, 4:5], in_=ident[:, 3:5], axis=AX.X, op=ALU.add)
-        nc.vector.tensor_copy(out=coefb[:, 0:5], in_=coef32[:, 0:5])
+        coef32 = const.tile([P, 4], F32, name="coef32")
+        coef = const.tile([P, 4], BF16, name="coef")
+        nc.vector.tensor_copy(out=coef32[:, 0:2], in_=ident[:, 0:2])
+        nc.vector.tensor_reduce(out=coef32[:, 2:3], in_=ident[:, 0:3], axis=AX.X, op=ALU.add)
+        nc.vector.tensor_reduce(out=coef32[:, 3:4], in_=ident[:, 1:3], axis=AX.X, op=ALU.add)
+        nc.vector.tensor_copy(out=coef[:], in_=coef32[:])
 
-        gam = [const.tile([P, N3], F32, name="gam%d" % w) for w in range(2)]
+        gam_w = const.tile([P, N3], F32, name="gam_w")
+        gam_u = const.tile([P, N3], F32, name="gam_u")
+        gam = (gam_w, gam_u)
         B01 = const.tile([P, 2 * H], F32, name="B01")
         B2 = const.tile([P, H], F32, name="B2")
         bU2 = const.tile([P, H], F32, name="bU2")
 
-        spread_count = [0]
+        def spread(vec, c, j):
+            ps = psum.tile([P, NB], F32, name="ps", tag="acc", bufs=6)
+            nc.tensor.matmul(out=ps[:], lhsT=coef[:, c:c + 1].to_broadcast([P, P]),
+                             rhs=vec[:, j * NB:(j + 1) * NB], start=True, stop=True)
+            return ps
 
-        def spread(dst, c, j0, nj, both=True):
-            for j in range(nj):
-                ps = psum.tile([P, NB], F32, name="ps", tag="acc", bufs=6)
-                nc.tensor.matmul(out=ps[:], lhsT=coefb[:, c:c + 1].to_broadcast([P, P]),
-                                 rhs=vecs[:, (j0 + j) * NB:(j0 + j + 1) * NB], start=True, stop=True)
-                if spread_count[0] % 2 == 0 or not both:
-                    nc.scalar.copy(out=dst[:, j * NB:(j + 1) * NB], in_=ps[:])
+        def spread_gamma(w):
+            for j in range(BANKS):
+                ps = spread(gvec, w, j)
+                if j % 2 == 0:
+                    nc.scalar.copy(out=gam[w][:, j * NB:(j + 1) * NB], in_=ps[:])
                 else:
-                    nc.vector.tensor_copy(out=dst[:, j * NB:(j + 1) * NB], in_=ps[:])
-                spread_count[0] += 1
+                    nc.vector.tensor_copy(out=gam[w][:, j * NB:(j + 1) * NB], in_=ps[:])
 
         codes = {}
         scls = {}
-
         groups = {}
 
         def prep_t(i, w):
             src32 = (x_sb[i] if w == 0 else h_sb[i])[:].bitcast(F32)
-            xt = psum.tile([P, NB], F32, name="xt", tag="xt", bufs=1)
+            xt = psum.tile([P, NB], F32, name="xt", tag="aux", bufs=2)
             for g in range(G):
                 for u in range(2):
                     nc.tensor.transpose(xt[:, (2 * g + u) * P:(2 * g + u + 1) * P],
@@ -132,10 +140,9 @@ def tile_lngrucell_kernel(tc, x_in, hx, W_words, W_scales, U_words, U_scales,
             groups[(i, w)] = grouped
 
         def prep_q(i, w):
-            grouped = groups[(i, w)]
             cd = const.tile([P, G * P], U32, name="codes%d_%d" % (w, i), align_bytes=64)
             sc = const.tile([P, G * P], U8, name="scl%d_%d" % (w, i), align_bytes=64)
-            nc.vector.quantize_mx(out=cd[:].bitcast(FP8X4), scales=sc[:], in_=grouped[:].bitcast(BF16))
+            nc.vector.quantize_mx(out=cd[:].bitcast(FP8X4), scales=sc[:], in_=groups[(i, w)][:].bitcast(BF16))
             codes[(i, w)] = cd
             scls[(i, w)] = sc
 
@@ -149,13 +156,21 @@ def tile_lngrucell_kernel(tc, x_in, hx, W_words, W_scales, U_words, U_scales,
                 start=start, stop=stop,
             )
 
+        def product(i, w, j):
+            acc = psum.tile([P, NB], F32, name="acc", tag="acc", bufs=6)
+            for g in range(G):
+                mx(acc, i, w, j, g, g == 0, g == G - 1)
+            return acc
+
         folds = {}
         mus = {}
         s2s = {}
         rss = {}
+        us = {}
+        ws = {}
 
         def fold(i, w):
-            f = psum.tile([P, NB], F32, name="fold", tag="fold", bufs=1)
+            f = psum.tile([P, NB], F32, name="fold", tag="aux", bufs=2)
             for j in range(BANKS):
                 for g in range(G):
                     mx(f, i, w, j, g, j == 0 and g == 0, j == BANKS - 1 and g == G - 1)
@@ -168,57 +183,102 @@ def tile_lngrucell_kernel(tc, x_in, hx, W_words, W_scales, U_words, U_scales,
                                  accum_out=mu[:])
             mus[(i, w)] = mu
 
-        def unit(i, w, dst):
-            mu = mus[(i, w)]
-            s2 = small.tile([P, BANKS], F32, name="s2", tag="s2")
-            for j in range(BANKS):
-                acc = psum.tile([P, NB], F32, name="acc", tag="acc", bufs=6)
-                for g in range(G):
-                    mx(acc, i, w, j, g, g == 0, g == G - 1)
-                junk = small.tile([P, NB], BF16, name="junk", tag="junk")
-                nc.scalar.activation(out=junk[:], in_=acc[:], func=ACT.Square, scale=-1.0, bias=mu[:, 0:1],
-                                     accum_out=s2[:, j:j + 1])
-                nc.vector.scalar_tensor_tensor(out=dst[:, j * NB:(j + 1) * NB], in0=acc[:], scalar=mu[:, 0:1],
-                                               in1=gam[w][:, j * NB:(j + 1) * NB], op0=ALU.subtract, op1=ALU.mult)
-            vs = small.tile([P, 1], F32, name="vs", tag="vs")
+        def scale_gamma(i, w, j, acc):
+            dst = us[i] if w == 0 else ws[i]
+            nc.vector.scalar_tensor_tensor(out=dst[:, j * NB:(j + 1) * NB], in0=acc[:], scalar=mus[(i, w)][:, 0:1],
+                                           in1=gam[w][:, j * NB:(j + 1) * NB], op0=ALU.subtract, op1=ALU.mult)
+
+        def unit_bank(i, w, j):
+            if j == 0:
+                s2s[(i, w)] = small.tile([P, BANKS], F32, name="s2", tag="s2")
+            acc = product(i, w, j)
+            scale_gamma(i, w, j, acc)
+            junk = small.tile([P, NB], BF16, name="junk", tag="junk")
+            nc.scalar.activation(out=junk[:], in_=acc[:], func=ACT.Square, scale=-1.0, bias=mus[(i, w)][:, 0:1],
+                                 accum_out=s2s[(i, w)][:, j:j + 1])
+
+        def rstd(i, w, vs):
             rs = small.tile([P, 1], F32, name="rs", tag="rs")
-            j6 = small.tile([P, BANKS], F32, name="j6", tag="j6")
-            nc.scalar.activation(out=j6[:], in_=s2[:], func=ACT.Identity, scale=1.0 / N3, bias=EPS / BANKS,
-                                 accum_out=vs[:])
             nc.gpsimd.tensor_tensor(out=rs[:], in0=vs[:], in1=mhalf[:], op=ALU.pow)
             rss[(i, w)] = rs
 
-        us = {}
-        ws = {}
+        def unit_end(i, w):
+            vs = small.tile([P, 1], F32, name="vs", tag="vs")
+            j6 = small.tile([P, BANKS], F32, name="j6", tag="j6")
+            nc.scalar.activation(out=j6[:], in_=s2s[(i, w)][:], func=ACT.Identity, scale=1.0 / N3, bias=EPS / BANKS,
+                                 accum_out=vs[:])
+            rstd(i, w, vs)
 
-        def cols(part, lo, hi):
+        def unit_first(i, w):
+            stats = small.tile([P, BANKS, 6], F32, name="stats", tag="stats")
+            mv = small.tile([P, 2], F32, name="mv", tag="mv")
+            vs = small.tile([P, 1], F32, name="vs", tag="vs")
+            accs = []
+            for j in range(BANKS):
+                acc = product(i, w, j)
+                nc.vector.bn_stats(out=stats[:, j, :], in_=acc[:])
+                accs.append(acc)
+            nc.vector.bn_aggr(out=mv[:], in_=stats[:].rearrange("p j s -> p (j s)"))
+            mus[(i, w)] = mv
+            for j in range(BANKS):
+                scale_gamma(i, w, j, accs[j])
+            nc.gpsimd.tensor_scalar(out=vs[:], in0=mv[:, 1:2], scalar1=EPS, scalar2=None, op0=ALU.add)
+            rstd(i, w, vs)
+
+        def cols(part, lo=0, hi=H):
             return slice(part * H + lo, part * H + hi)
 
-        def scale_a(i, part, lo=0, hi=H):
-            bias = B2[:, lo:hi] if part == 2 else B01[:, cols(part, lo, hi)]
-            u = us[i][:, cols(part, lo, hi)]
+        def scale_a(i, part):
+            bias = B2[:] if part == 2 else B01[:, cols(part)]
+            u = us[i][:, cols(part)]
             nc.vector.scalar_tensor_tensor(out=u, in0=u, scalar=rss[(i, 0)][:, 0:1], in1=bias,
                                            op0=ALU.mult, op1=ALU.add)
 
-        def add_c(i, part, lo=0, hi=H):
-            u = us[i][:, cols(part, lo, hi)]
-            nc.vector.scalar_tensor_tensor(out=u, in0=ws[i][:, cols(part, lo, hi)], scalar=rss[(i, 1)][:, 0:1], in1=u,
+        def hu2(i):
+            t = ws[i][:, cols(2)]
+            nc.vector.scalar_tensor_tensor(out=t, in0=t, scalar=rss[(i, 1)][:, 0:1], in1=bU2[:],
                                            op0=ALU.mult, op1=ALU.add)
 
-        def hu2(i, lo=0, hi=H):
-            t = ws[i][:, cols(2, lo, hi)]
-            nc.vector.scalar_tensor_tensor(out=t, in0=t, scalar=rss[(i, 1)][:, 0:1], in1=bU2[:, lo:hi],
+        def scale_ps(i, part):
+            banks = []
+            for k, (lo, hi) in enumerate(HALVES):
+                ps = spread(bvec, 3 if part == 2 else 2, 2 * part + k)
+                u = us[i][:, cols(part, lo, hi)]
+                nc.vector.scalar_tensor_tensor(out=u, in0=u, scalar=rss[(i, 0)][:, 0:1], in1=ps[:],
+                                               op0=ALU.mult, op1=ALU.add)
+                banks.append(ps)
+            return banks
+
+        def hu2_ps(i):
+            banks = []
+            for k, (lo, hi) in enumerate(HALVES):
+                ps = spread(bvec, 0, 4 + k)
+                t = ws[i][:, cols(2, lo, hi)]
+                nc.vector.scalar_tensor_tensor(out=t, in0=t, scalar=rss[(i, 1)][:, 0:1], in1=ps[:],
+                                               op0=ALU.mult, op1=ALU.add)
+                banks.append(ps)
+            return banks
+
+        def keep(banks, dst):
+            for ps, (lo, hi) in zip(banks, HALVES):
+                nc.scalar.copy(out=dst[:, lo:hi], in_=ps[:])
+
+        def add_c(i, part):
+            u = us[i][:, cols(part)]
+            nc.vector.scalar_tensor_tensor(out=u, in0=ws[i][:, cols(part)], scalar=rss[(i, 1)][:, 0:1], in1=u,
                                            op0=ALU.mult, op1=ALU.add)
 
         def gate(i, part, lo=0, hi=H):
             u = us[i][:, cols(part, lo, hi)]
             nc.scalar.activation(out=u, in_=u, func=ACT.Tanh if part == 2 else ACT.Sigmoid)
 
-        def cand(eng, i, lo=0, hi=H):
+        def cand_mul(eng, i, lo, hi):
             t = ws[i][:, cols(2, lo, hi)]
-            n = us[i][:, cols(2, lo, hi)]
             eng.tensor_tensor(out=t, in0=us[i][:, cols(1, lo, hi)], in1=t, op=ALU.mult)
-            eng.tensor_tensor(out=n, in0=t, in1=n, op=ALU.add)
+
+        def cand_add(eng, i, lo, hi):
+            n = us[i][:, cols(2, lo, hi)]
+            eng.tensor_tensor(out=n, in0=ws[i][:, cols(2, lo, hi)], in1=n, op=ALU.add)
 
         def blend_d(eng, i, lo=0, hi=H):
             eng.tensor_tensor(out=ws[i][:, cols(2, lo, hi)], in0=h_sb[i][:, lo:hi], in1=us[i][:, cols(2, lo, hi)],
@@ -228,69 +288,116 @@ def tile_lngrucell_kernel(tc, x_in, hx, W_words, W_scales, U_words, U_scales,
             t = ws[i][:, cols(2, lo, hi)]
             eng.tensor_tensor(out=t, in0=us[i][:, cols(0, lo, hi)], in1=t, op=ALU.mult)
 
+        def store(i, lo, hi):
+            nc.sync.dma_start(out=out[i * P:(i + 1) * P, lo:hi], in_=ws[i][:, cols(2, lo, hi)])
+
         def blend_o(eng, i, lo=0, hi=H):
             t = ws[i][:, cols(2, lo, hi)]
             eng.tensor_tensor(out=t, in0=t, in1=us[i][:, cols(2, lo, hi)], op=ALU.add)
-            nc.sync.dma_start(out=out[i * P:(i + 1) * P, lo:hi], in_=t)
+            store(i, lo, hi)
 
-        halves = ((0, H // 2), (H // 2, H))
-        spread(gam[0], 0, 0, BANKS)
-        prep_t(0, 0)
-        prep_q(0, 0)
-        spread(B01, 3, 0, 4)
-        spread(B2, 4, 4, 2)
-        prep_t(0, 1)
-        prep_q(0, 1)
-        fold(0, 0)
-        mean(0, 0)
+        def blend_zh(i):
+            nc.vector.tensor_tensor(out=ws[i][:, cols(0)], in0=us[i][:, cols(0)], in1=h_sb[i][:], op=ALU.mult)
+
+        def blend_zn(i, lo, hi):
+            t = ws[i][:, cols(2, lo, hi)]
+            nc.vector.scalar_tensor_tensor(out=t, in0=us[i][:, cols(0, lo, hi)], scalar=1.0,
+                                           in1=us[i][:, cols(2, lo, hi)], op0=ALU.subtract, op1=ALU.mult)
+
+        def blend_s(i, lo, hi):
+            t = ws[i][:, cols(2, lo, hi)]
+            nc.vector.tensor_tensor(out=t, in0=ws[i][:, cols(0, lo, hi)], in1=t, op=ALU.subtract)
+            store(i, lo, hi)
+
         for i in range(BT):
             us[i] = work.tile([P, N3], F32, name="u", tag="u")
             ws[i] = work.tile([P, N3], F32, name="wt", tag="wt")
-            unit(i, 0, us[i])
             if i == 0:
-                spread(gam[1], 1, 0, BANKS)
-            if i + 1 < BT:
-                prep_t(i + 1, 0)
-            fold(i, 1)
-            if i > 0:
-                gate(i - 1, 0)
-                for lo, hi in halves:
-                    gate(i - 1, 2, lo, hi)
-                for lo, hi in halves:
-                    blend_d(nc.gpsimd, i - 1, lo, hi)
-                for lo, hi in halves:
-                    blend_e(nc.gpsimd, i - 1, lo, hi)
-            mean(i, 1)
-            if i == 0:
-                scale_a(i, 1)
-                scale_a(i, 2)
-                scale_a(i, 0)
-            if i + 1 < BT:
-                prep_q(i + 1, 0)
-            unit(i, 1, ws[i])
-            if i == 0:
-                spread(bU2, 2, 4, 2, both=False)
-            if i + 1 < BT:
-                prep_t(i + 1, 1)
-                prep_q(i + 1, 1)
-                fold(i + 1, 0)
-                mean(i + 1, 0)
-            if i > 0:
-                blend_o(nc.vector, i - 1)
-                scale_a(i, 1)
-                scale_a(i, 2)
-            add_c(i, 1)
-            gate(i, 1)
-            hu2(i)
-            if i > 0:
-                scale_a(i, 0)
-            add_c(i, 0)
-            cand(nc.vector, i)
+                prep_t(0, 0)
+                prep_q(0, 0)
+                spread_gamma(0)
+                spread_gamma(1)
+                prep_t(0, 1)
+                prep_q(0, 1)
+                unit_first(0, 0)
+                fold(0, 1)
+                mean(0, 1)
+                prep_t(1, 0)
+                prep_q(1, 0)
+                for j in range(BANKS):
+                    unit_bank(0, 1, j)
+                unit_end(0, 1)
+                r_banks = scale_ps(0, 1)
+                prep_t(1, 1)
+                prep_q(1, 1)
+                n_banks = scale_ps(0, 2)
+                fold(1, 0)
+                keep(r_banks, B01[:, cols(1)])
+                mean(1, 0)
+                keep(n_banks, B2)
+                add_c(0, 1)
+                z_banks = scale_ps(0, 0)
+                fold(1, 1)
+                gate(0, 1)
+                keep(z_banks, B01[:, cols(0)])
+                add_c(0, 0)
+                mean(1, 1)
+                gate(0, 0)
+                keep(hu2_ps(0), bU2)
+            else:
+                for lo, hi in HALVES:
+                    cand_mul(nc.gpsimd, i - 1, lo, hi)
+                for lo, hi in HALVES:
+                    cand_add(nc.gpsimd, i - 1, lo, hi)
+                for j in range(BANKS):
+                    unit_bank(i, 0, j)
+                    if j >= BANKS - 2:
+                        lo, hi = HALVES[j - BANKS + 2]
+                        gate(i - 1, 2, lo, hi)
+                        blend_d(nc.gpsimd, i - 1, lo, hi)
+                unit_end(i, 0)
+                if i + 1 < BT:
+                    prep_t(i + 1, 0)
+                    prep_t(i + 1, 1)
+                for j in range(BANKS):
+                    unit_bank(i, 1, j)
+                if i + 1 == BT:
+                    for lo, hi in HALVES:
+                        blend_e(nc.gpsimd, i - 1, lo, hi)
+                unit_end(i, 1)
+                if i + 1 < BT:
+                    prep_q(i + 1, 0)
+                    prep_q(i + 1, 1)
+                    fold(i + 1, 0)
+                    mean(i + 1, 0)
+                    fold(i + 1, 1)
+                    scale_a(i, 1)
+                    blend_e(nc.vector, i - 1)
+                    blend_o(nc.vector, i - 1)
+                    scale_a(i, 2)
+                    add_c(i, 1)
+                    gate(i, 1)
+                    mean(i + 1, 1)
+                    scale_a(i, 0)
+                    add_c(i, 0)
+                    gate(i, 0)
+                    hu2(i)
         last = BT - 1
+        for lo, hi in HALVES:
+            blend_o(nc.gpsimd, last - 1, lo, hi)
+        scale_ps(last, 1)
+        scale_ps(last, 2)
+        scale_ps(last, 0)
+        hu2_ps(last)
+        add_c(last, 1)
+        gate(last, 1)
+        add_c(last, 0)
         gate(last, 0)
-        for lo, hi in halves:
+        for lo, hi in HALVES:
+            cand_mul(nc.vector, last, lo, hi)
+            cand_add(nc.vector, last, lo, hi)
             gate(last, 2, lo, hi)
-        for lo, hi in halves:
-            blend_d(nc.vector, last, lo, hi)
-            blend_e(nc.vector, last, lo, hi)
-            blend_o(nc.vector, last, lo, hi)
+        blend_zh(last)
+        for lo, hi in HALVES:
+            blend_zn(last, lo, hi)
+            blend_s(last, lo, hi)

@@ -59,11 +59,14 @@ def tile_lngrucell_kernel(tc, x_in, hx, W_words, W_scales, U_words, U_scales,
             nc.sync.dma_start(out=dst[i][:], in_=src[i * P:(i + 1) * P, :])
 
         def load_scales(w, src):
-            for r in range(4):
-                nc.sync.dma_start(
-                    out=planes[w][r:P:32, :, :].bitcast(I32),
-                    in_=src[:, r:16:4, :].rearrange("g q n -> q g n").bitcast(I32),
-                )
+            for half in range(2):
+                for r in range(4):
+                    p0 = 32 * half + r
+                    q0 = 4 * half + r
+                    nc.sync.dma_start(
+                        out=planes[w][p0:P:64, :, :].bitcast(I32),
+                        in_=src[:, q0:16:8, :].rearrange("g q n -> q g n").bitcast(I32),
+                    )
 
         def load_words(w, src, chunks):
             step = 2 * N3 // chunks

@@ -48,12 +48,12 @@ def tile_lngrucell_kernel(tc, x_in, hx, W_words, W_scales, U_words, U_scales,
         x_sb = [const.tile([P, H], BF16, name="x_sb%d" % i) for i in range(BT)]
         h_sb = [const.tile([P, H], BF16, name="h_sb%d" % i) for i in range(BT)]
 
-        make_identity(nc, ident[:])
-        nc.vector.memset(mhalf[:], -0.5)
         nc.vector.memset(gvec[:].bitcast(I32), 0)
         nc.vector.memset(planes[0][:].rearrange("p g n -> p (g n)").bitcast(I32), 0)
-        nc.vector.memset(planes[1][:].rearrange("p g n -> p (g n)").bitcast(I32), 0)
-        nc.vector.memset(bvec[:].bitcast(I32), 0)
+        nc.vector.memset(mhalf[:], -0.5)
+        make_identity(nc, ident[:])
+        nc.gpsimd.memset(planes[1][:].rearrange("p g n -> p (g n)").bitcast(I32), 0)
+        nc.gpsimd.memset(bvec[:].bitcast(I32), 0)
 
         def load_rows(dst, src, i):
             nc.sync.dma_start(out=dst[i][:], in_=src[i * P:(i + 1) * P, :])
@@ -375,13 +375,13 @@ def tile_lngrucell_kernel(tc, x_in, hx, W_words, W_scales, U_words, U_scales,
                     mean(i + 1, 0)
                     fold(i + 1, 1)
                     scale_a(i, 1)
+                    scale_a(i, 0)
                     blend_e(nc.vector, i - 1)
-                    blend_o(nc.vector, i - 1)
                     scale_a(i, 2)
+                    blend_o(nc.vector, i - 1)
                     add_c(i, 1)
                     gate(i, 1)
                     mean(i + 1, 1)
-                    scale_a(i, 0)
                     add_c(i, 0)
                     gate(i, 0)
                     hu2(i)
@@ -398,9 +398,11 @@ def tile_lngrucell_kernel(tc, x_in, hx, W_words, W_scales, U_words, U_scales,
         gate(last, 0)
         for lo, hi in HALVES:
             cand_mul(nc.vector, last, lo, hi)
+        for lo, hi in HALVES:
             cand_add(nc.vector, last, lo, hi)
             gate(last, 2, lo, hi)
         blend_zh(last)
         for lo, hi in HALVES:
             blend_zn(last, lo, hi)
+        for lo, hi in HALVES:
             blend_s(last, lo, hi)

@@ -40,89 +40,93 @@ def tile_lngrucell_kernel(tc, x_in, hx, W_words, W_scales, U_words, U_scales,
 
         planes = [const.tile([P, G, N3], U8, name="plane%d" % w, align_bytes=64) for w in range(2)]
         words = [const.tile([P, G, 2 * N3], U8, name="words%d" % w, align_bytes=64) for w in range(2)]
-        gvec = const.tile([P, N3], BF16, name="gvec")
-        bvec = const.tile([P, N3], BF16, name="bvec")
+        gvec = [const.tile([P, N3 // 2], BF16, name="gvec%d" % w) for w in range(1)]
+        gam_u = const.tile([P, N3], BF16, name="gam_u")
+        bvec = const.tile([P, N3 // 2], BF16, name="bvec")
         mhalf = const.tile([P, 1], F32, name="mhalf")
         warm = const.tile([P, 1], F32, name="warm")
         ident = const.tile([P, P], F32, name="ident")
         x_sb = [const.tile([P, H], BF16, name="x_sb%d" % i) for i in range(BT)]
         h_sb = [const.tile([P, H], BF16, name="h_sb%d" % i) for i in range(BT)]
 
-        nc.vector.memset(gvec[:].bitcast(I32), 0)
         nc.vector.memset(planes[0][:].rearrange("p g n -> p (g n)").bitcast(I32), 0)
+        nc.vector.memset(gvec[0][:].bitcast(I32), 0)
         nc.vector.memset(mhalf[:], -0.5)
         make_identity(nc, ident[:])
-        nc.gpsimd.memset(planes[1][:].rearrange("p g n -> p (g n)").bitcast(I32), 0)
-        nc.gpsimd.memset(bvec[:].bitcast(I32), 0)
+
+        coef32 = const.tile([P, 5], F32, name="coef32")
+        coef = const.tile([P, 5], BF16, name="coef")
+        nc.vector.tensor_copy(out=coef32[:, 0:2], in_=ident[:, 0:2])
+        for c, first in ((2, 0), (3, 1), (4, 3)):
+            nc.vector.tensor_reduce(out=coef32[:, c:c + 1], in_=ident[:, first:6:2], axis=AX.X, op=ALU.add)
+        nc.vector.memset(planes[1][:].rearrange("p g n -> p (g n)").bitcast(I32), 0)
+        nc.vector.tensor_copy(out=coef[:], in_=coef32[:])
+        nc.vector.memset(bvec[:].bitcast(I32), 0)
 
         def load_rows(dst, src, i):
             nc.sync.dma_start(out=dst[i][:], in_=src[i * P:(i + 1) * P, :])
 
-        def load_scales(w, src):
-            for half in range(2):
-                for r in range(4):
-                    p0 = 32 * half + r
-                    q0 = 4 * half + r
-                    nc.sync.dma_start(
-                        out=planes[w][p0:P:64, :, :].bitcast(I32),
-                        in_=src[:, q0:16:8, :].rearrange("g q n -> q g n").bitcast(I32),
-                    )
-
-        def load_words(w, src, chunks):
-            step = 2 * N3 // chunks
-            for c in range(chunks):
+        def load_scales(w, src, first, last):
+            for r in range(first, last):
                 nc.sync.dma_start(
-                    out=words[w][:, :, c * step:(c + 1) * step].bitcast(I32),
-                    in_=src[:, :, c * step:(c + 1) * step].rearrange("g p c -> p g c").bitcast(I32),
+                    out=planes[w][r:P:32, :, :].bitcast(I32),
+                    in_=src[:, r:16:4, :].rearrange("g q n -> q g n").bitcast(I32),
                 )
 
-        def load_vec(eng, dst, r, v):
-            eng.dma_start(out=dst[r:r + 1, :], in_=v.rearrange("(o n) -> o n", o=1))
+        def load_words(w, src, half):
+            nc.sync.dma_start(
+                out=words[w][:, :, half * N3:(half + 1) * N3].bitcast(I32),
+                in_=src[:, :, half * N3:(half + 1) * N3].rearrange("g p c -> p g c").bitcast(I32),
+            )
 
-        load_rows(x_sb, x_in, 0)
-        load_rows(h_sb, hx, 0)
-        load_vec(nc.scalar, gvec, 0, W_gamma)
-        load_vec(nc.scalar, gvec, 1, U_gamma)
+        def load_vec(dst, v, src):
+            nc.sync.dma_start(out=dst[2 * v:2 * v + 2, :], in_=src.rearrange("(k n) -> k n", k=2))
+
         nc.scalar.activation(out=warm[:], in_=mhalf[:], func=ACT.Sigmoid)
-        load_scales(0, W_scales)
-        load_words(0, W_words, 2)
-        load_scales(1, U_scales)
-        load_words(1, U_words, 2)
+        load_rows(x_sb, x_in, 0)
+        load_scales(0, W_scales, 0, 4)
+        load_vec(gvec[0], 0, W_gamma)
+        load_words(0, W_words, 0)
+        load_rows(h_sb, hx, 0)
+        load_words(0, W_words, 1)
         load_rows(x_sb, x_in, 1)
+        for v, src in enumerate((U_beta, W_beta, b)):
+            load_vec(bvec, v, src)
+        load_scales(1, U_scales, 0, 1)
+        load_words(1, U_words, 0)
+        load_words(1, U_words, 1)
+        load_scales(1, U_scales, 1, 4)
+        nc.sync.dma_start(out=gam_u[:], in_=U_gamma.partition_broadcast(P))
         load_rows(h_sb, hx, 1)
-        for r, v in enumerate((U_beta, W_beta, b)):
-            load_vec(nc.sync, bvec, r, v)
         for i in range(2, BT):
             load_rows(x_sb, x_in, i)
             load_rows(h_sb, hx, i)
 
-        coef32 = const.tile([P, 4], F32, name="coef32")
-        coef = const.tile([P, 4], BF16, name="coef")
-        nc.vector.tensor_copy(out=coef32[:, 0:2], in_=ident[:, 0:2])
-        nc.vector.tensor_reduce(out=coef32[:, 2:3], in_=ident[:, 0:3], axis=AX.X, op=ALU.add)
-        nc.vector.tensor_reduce(out=coef32[:, 3:4], in_=ident[:, 1:3], axis=AX.X, op=ALU.add)
-        nc.vector.tensor_copy(out=coef[:], in_=coef32[:])
-
         gam_w = const.tile([P, N3], F32, name="gam_w")
-        gam_u = const.tile([P, N3], F32, name="gam_u")
         gam = (gam_w, gam_u)
         B01 = const.tile([P, 2 * H], F32, name="B01")
         B2 = const.tile([P, H], F32, name="B2")
         bU2 = const.tile([P, H], F32, name="bU2")
 
-        def spread(vec, c, j):
-            ps = psum.tile([P, NB], F32, name="ps", tag="acc", bufs=6)
+        def spread(vec, c, j, tag="acc"):
+            ps = psum.tile([P, NB], F32, name="ps", tag=tag, bufs=6 if tag == "acc" else 2)
+            k = j % 3
             nc.tensor.matmul(out=ps[:], lhsT=coef[:, c:c + 1].to_broadcast([P, P]),
-                             rhs=vec[:, j * NB:(j + 1) * NB], start=True, stop=True)
+                             rhs=vec[:, k * NB:(k + 1) * NB], start=True, stop=True)
             return ps
 
         def spread_gamma(w):
             for j in range(BANKS):
-                ps = spread(gvec, w, j)
-                if j % 2 == 0:
-                    nc.scalar.copy(out=gam[w][:, j * NB:(j + 1) * NB], in_=ps[:])
-                else:
+                ps = spread(gvec[w], j // 3, j, "acc" if w == 0 else "aux")
+                if w == 0 and j % 2:
                     nc.vector.tensor_copy(out=gam[w][:, j * NB:(j + 1) * NB], in_=ps[:])
+                else:
+                    nc.scalar.copy(out=gam[w][:, j * NB:(j + 1) * NB], in_=ps[:])
+
+        def table(j):
+            ps = spread(bvec, 4 if j > 3 else 2 + j // 3, j, "aux")
+            dst = B2[:, (j - 4) * NB:(j - 3) * NB] if j > 3 else B01[:, j * NB:(j + 1) * NB]
+            nc.scalar.copy(out=dst, in_=ps[:])
 
         codes = {}
         scls = {}
@@ -191,10 +195,11 @@ def tile_lngrucell_kernel(tc, x_in, hx, W_words, W_scales, U_words, U_scales,
             nc.vector.scalar_tensor_tensor(out=dst[:, j * NB:(j + 1) * NB], in0=acc[:], scalar=mus[(i, w)][:, 0:1],
                                            in1=gam[w][:, j * NB:(j + 1) * NB], op0=ALU.subtract, op1=ALU.mult)
 
-        def unit_bank(i, w, j):
+        def unit_bank(i, w, j, acc=None):
             if j == 0:
                 s2s[(i, w)] = small.tile([P, BANKS], F32, name="s2", tag="s2")
-            acc = product(i, w, j)
+            if acc is None:
+                acc = product(i, w, j)
             scale_gamma(i, w, j, acc)
             junk = small.tile([P, NB], BF16, name="junk", tag="junk")
             nc.scalar.activation(out=junk[:], in_=acc[:], func=ACT.Square, scale=-1.0, bias=mus[(i, w)][:, 0:1],
@@ -212,21 +217,22 @@ def tile_lngrucell_kernel(tc, x_in, hx, W_words, W_scales, U_words, U_scales,
                                  accum_out=vs[:])
             rstd(i, w, vs)
 
-        def unit_first(i, w):
+        def first_stats(w, beside):
             stats = small.tile([P, BANKS, 6], F32, name="stats", tag="stats")
             mv = small.tile([P, 2], F32, name="mv", tag="mv")
             vs = small.tile([P, 1], F32, name="vs", tag="vs")
             accs = []
             for j in range(BANKS):
-                acc = product(i, w, j)
+                acc = product(0, w, j)
                 nc.vector.bn_stats(out=stats[:, j, :], in_=acc[:])
                 accs.append(acc)
+                for f in beside.get(j, ()):
+                    f()
             nc.vector.bn_aggr(out=mv[:], in_=stats[:].rearrange("p j s -> p (j s)"))
-            mus[(i, w)] = mv
-            for j in range(BANKS):
-                scale_gamma(i, w, j, accs[j])
+            mus[(0, w)] = mv
             nc.gpsimd.tensor_scalar(out=vs[:], in0=mv[:, 1:2], scalar1=EPS, scalar2=None, op0=ALU.add)
-            rstd(i, w, vs)
+            rstd(0, w, vs)
+            return accs
 
         def cols(part, lo=0, hi=H):
             return slice(part * H + lo, part * H + hi)
@@ -237,6 +243,19 @@ def tile_lngrucell_kernel(tc, x_in, hx, W_words, W_scales, U_words, U_scales,
             nc.vector.scalar_tensor_tensor(out=u, in0=u, scalar=rss[(i, 0)][:, 0:1], in1=bias,
                                            op0=ALU.mult, op1=ALU.add)
 
+        def scale_g(part):
+            u = us[0][:, cols(part)]
+            nc.gpsimd.tensor_scalar(out=u, in0=u, scalar1=rss[(0, 0)][:, 0:1], scalar2=0.0, op0=ALU.mult, op1=ALU.add)
+
+        def scale_s(part):
+            u = us[0][:, cols(part)]
+            nc.scalar.activation(out=u, in_=u, func=ACT.Identity, scale=rss[(0, 0)][:, 0:1])
+
+        def bias_g(part, bias):
+            for lo, hi in HALVES:
+                u = us[0][:, cols(part, lo, hi)]
+                nc.gpsimd.tensor_tensor(out=u, in0=u, in1=bias[:, lo:hi], op=ALU.add)
+
         def hu2(i):
             t = ws[i][:, cols(2)]
             nc.vector.scalar_tensor_tensor(out=t, in0=t, scalar=rss[(i, 1)][:, 0:1], in1=bU2[:],
@@ -245,7 +264,8 @@ def tile_lngrucell_kernel(tc, x_in, hx, W_words, W_scales, U_words, U_scales,
         def scale_ps(i, part):
             banks = []
             for k, (lo, hi) in enumerate(HALVES):
-                ps = spread(bvec, 3 if part == 2 else 2, 2 * part + k)
+                j = 2 * part + k
+                ps = spread(bvec, 4 if part == 2 else 2 + j // 3, j)
                 u = us[i][:, cols(part, lo, hi)]
                 nc.vector.scalar_tensor_tensor(out=u, in0=u, scalar=rss[(i, 0)][:, 0:1], in1=ps[:],
                                                op0=ALU.mult, op1=ALU.add)
@@ -255,7 +275,7 @@ def tile_lngrucell_kernel(tc, x_in, hx, W_words, W_scales, U_words, U_scales,
         def hu2_ps(i):
             banks = []
             for k, (lo, hi) in enumerate(HALVES):
-                ps = spread(bvec, 0, 4 + k)
+                ps = spread(bvec, 1, 4 + k)
                 t = ws[i][:, cols(2, lo, hi)]
                 nc.vector.scalar_tensor_tensor(out=t, in0=t, scalar=rss[(i, 1)][:, 0:1], in1=ps[:],
                                                op0=ALU.mult, op1=ALU.add)
@@ -319,32 +339,31 @@ def tile_lngrucell_kernel(tc, x_in, hx, W_words, W_scales, U_words, U_scales,
                 prep_t(0, 0)
                 prep_q(0, 0)
                 spread_gamma(0)
-                spread_gamma(1)
                 prep_t(0, 1)
                 prep_q(0, 1)
-                unit_first(0, 0)
-                fold(0, 1)
-                mean(0, 1)
-                prep_t(1, 0)
-                prep_q(1, 0)
+                accs = first_stats(0, {
+                    3: (lambda: prep_t(1, 0), lambda: table(0)), 4: (lambda: table(1),),
+                    5: (lambda: prep_q(1, 0), lambda: table(2), lambda: table(3))})
                 for j in range(BANKS):
-                    unit_bank(0, 1, j)
-                unit_end(0, 1)
-                r_banks = scale_ps(0, 1)
+                    scale_gamma(0, 0, j, accs[j])
+                table(4)
+                table(5)
+                scale_g(0)
+                scale_s(1)
+                scale_s(2)
+                bias_g(0, B01[:, cols(0)])
+                bias_g(1, B01[:, cols(1)])
+                accs = first_stats(1, {})
+                bias_g(2, B2)
                 prep_t(1, 1)
-                prep_q(1, 1)
-                n_banks = scale_ps(0, 2)
+                for j in range(BANKS):
+                    scale_gamma(0, 1, j, accs[j])
                 fold(1, 0)
-                keep(r_banks, B01[:, cols(1)])
                 mean(1, 0)
-                keep(n_banks, B2)
+                prep_q(1, 1)
                 add_c(0, 1)
-                z_banks = scale_ps(0, 0)
-                fold(1, 1)
                 gate(0, 1)
-                keep(z_banks, B01[:, cols(0)])
                 add_c(0, 0)
-                mean(1, 1)
                 gate(0, 0)
                 keep(hu2_ps(0), bU2)
             else:
@@ -352,8 +371,13 @@ def tile_lngrucell_kernel(tc, x_in, hx, W_words, W_scales, U_words, U_scales,
                     cand_mul(nc.gpsimd, i - 1, lo, hi)
                 for lo, hi in HALVES:
                     cand_add(nc.gpsimd, i - 1, lo, hi)
+                early = []
+                if i == 1:
+                    early = [product(1, 0, j) for j in range(4)]
+                    fold(1, 1)
+                    mean(1, 1)
                 for j in range(BANKS):
-                    unit_bank(i, 0, j)
+                    unit_bank(i, 0, j, early[j] if j < len(early) else None)
                     if j >= BANKS - 2:
                         lo, hi = HALVES[j - BANKS + 2]
                         gate(i - 1, 2, lo, hi)

@@ -23,6 +23,7 @@ BANKS = N3 // NB
 G = H // 512
 BT = B // P
 EPS = 1e-5
+WARM = 5
 FLOPS = 2 * 2 * B * H * N3
 HALVES = ((0, NB), (NB, H))
 
@@ -32,36 +33,41 @@ def tile_lngrucell_kernel(tc, x_in, hx, W_words, W_scales, U_words, U_scales,
     nc = tc.nc
     with ExitStack() as ctx:
         const = ctx.enter_context(tc.tile_pool(name="const", bufs=1))
-        xin = ctx.enter_context(tc.tile_pool(name="xin", bufs=2))
+        xin = ctx.enter_context(tc.tile_pool(name="xin", bufs=4))
         work = ctx.enter_context(tc.tile_pool(name="work", bufs=3))
         small = ctx.enter_context(tc.tile_pool(name="small", bufs=4))
         psum = ctx.enter_context(tc.psum_pool(name="psum", bufs=1))
         ctx.enter_context(tc.manual_schedule())
 
         planes = [const.tile([P, G, N3], U8, name="plane%d" % w, align_bytes=64) for w in range(2)]
-        words = [const.tile([P, G, 2 * N3], U8, name="words%d" % w, align_bytes=64) for w in range(2)]
-        gvec = [const.tile([P, N3 // 2], BF16, name="gvec%d" % w) for w in range(1)]
-        gam_u = const.tile([P, N3], BF16, name="gam_u")
-        bvec = const.tile([P, N3 // 2], BF16, name="bvec")
+        chunks = (((0,2),(2,6)), ((0,3),(3,6)))
+        words = [[const.tile([P, G, 2 * NB * (last - first)], U8, name="words%d_%d" % (w, first), align_bytes=64)
+                  for first, last in chunks[w]] for w in range(2)]
+        gvec = const.tile([P, NB], BF16, name="gvec")
+        gam = [const.tile([P, N3], BF16, name="gam%d" % w) for w in range(2)]
+        bvec = const.tile([P, NB], BF16, name="bvec")
         mhalf = const.tile([P, 1], F32, name="mhalf")
         warm = const.tile([P, 1], F32, name="warm")
         ident = const.tile([P, P], F32, name="ident")
+        cold = const.tile([P, NB], BF16, name="cold")
+        diag = const.tile([P, P], F32, name="diag")
         x_sb = [const.tile([P, H], BF16, name="x_sb%d" % i) for i in range(BT)]
         h_sb = [const.tile([P, H], BF16, name="h_sb%d" % i) for i in range(BT)]
 
+        nc.vector.memset(cold[:].bitcast(I32), 0)
+        nc.vector.memset(gvec[:].bitcast(I32), 0)
         nc.vector.memset(planes[0][:].rearrange("p g n -> p (g n)").bitcast(I32), 0)
-        nc.vector.memset(gvec[0][:].bitcast(I32), 0)
+        nc.vector.memset(bvec[:].bitcast(I32), 0)
         nc.vector.memset(mhalf[:], -0.5)
         make_identity(nc, ident[:])
 
-        coef32 = const.tile([P, 5], F32, name="coef32")
-        coef = const.tile([P, 5], BF16, name="coef")
-        nc.vector.tensor_copy(out=coef32[:, 0:2], in_=ident[:, 0:2])
-        for c, first in ((2, 0), (3, 1), (4, 3)):
-            nc.vector.tensor_reduce(out=coef32[:, c:c + 1], in_=ident[:, first:6:2], axis=AX.X, op=ALU.add)
+        coef32 = const.tile([P, BANKS], F32, name="coef32")
+        coef = const.tile([P, 5 * BANKS], BF16, name="coef")
+        nc.vector.tensor_copy(out=coef[:, 0:4 * BANKS], in_=ident[:, 0:4 * BANKS])
+        nc.vector.tensor_tensor(out=coef32[:], in0=ident[:, BANKS:2 * BANKS], in1=ident[:, 2 * BANKS:3 * BANKS], op=ALU.add)
         nc.vector.memset(planes[1][:].rearrange("p g n -> p (g n)").bitcast(I32), 0)
-        nc.vector.tensor_copy(out=coef[:], in_=coef32[:])
-        nc.vector.memset(bvec[:].bitcast(I32), 0)
+        nc.vector.tensor_tensor(out=coef[:, 4 * BANKS:4 * BANKS + 4], in0=coef32[:, 0:4], in1=ident[:, 0:4], op=ALU.add)
+        nc.vector.tensor_copy(out=coef[:, 4 * BANKS + 4:5 * BANKS], in_=coef32[:, 4:BANKS])
 
         def load_rows(dst, src, i):
             nc.sync.dma_start(out=dst[i][:], in_=src[i * P:(i + 1) * P, :])
@@ -73,58 +79,55 @@ def tile_lngrucell_kernel(tc, x_in, hx, W_words, W_scales, U_words, U_scales,
                     in_=src[:, r:16:4, :].rearrange("g q n -> q g n").bitcast(I32),
                 )
 
-        def load_words(w, src, half):
-            nc.sync.dma_start(
-                out=words[w][:, :, half * N3:(half + 1) * N3].bitcast(I32),
-                in_=src[:, :, half * N3:(half + 1) * N3].rearrange("g p c -> p g c").bitcast(I32),
-            )
+        def load_words(w, src):
+            for tile, (first, last) in zip(words[w], chunks[w]):
+                nc.sync.dma_start(
+                    out=tile[:].bitcast(I32),
+                    in_=src[:, :, 2 * NB * first:2 * NB * last].rearrange("g p c -> p g c").bitcast(I32))
 
         def load_vec(dst, v, src):
-            nc.sync.dma_start(out=dst[2 * v:2 * v + 2, :], in_=src.rearrange("(k n) -> k n", k=2))
+            nc.gpsimd.dma_start(out=dst[BANKS * v:BANKS * (v + 1), :], in_=src.rearrange("(j n) -> j n", n=NB))
 
         nc.scalar.activation(out=warm[:], in_=mhalf[:], func=ACT.Sigmoid)
+        load_vec(gvec, 0, W_gamma)
+        for v, src in enumerate((U_beta, W_beta, b, U_gamma)):
+            load_vec(bvec, v, src)
         load_rows(x_sb, x_in, 0)
         load_scales(0, W_scales, 0, 4)
-        load_vec(gvec[0], 0, W_gamma)
-        load_words(0, W_words, 0)
+        load_words(0, W_words)
+        load_scales(1, U_scales, 0, 4)
         load_rows(h_sb, hx, 0)
-        load_words(0, W_words, 1)
         load_rows(x_sb, x_in, 1)
-        for v, src in enumerate((U_beta, W_beta, b)):
-            load_vec(bvec, v, src)
-        load_scales(1, U_scales, 0, 1)
-        load_words(1, U_words, 0)
-        load_words(1, U_words, 1)
-        load_scales(1, U_scales, 1, 4)
-        nc.sync.dma_start(out=gam_u[:], in_=U_gamma.partition_broadcast(P))
+        load_words(1, U_words)
         load_rows(h_sb, hx, 1)
         for i in range(2, BT):
             load_rows(x_sb, x_in, i)
             load_rows(h_sb, hx, i)
 
-        gam_w = const.tile([P, N3], F32, name="gam_w")
-        gam = (gam_w, gam_u)
         B01 = const.tile([P, 2 * H], F32, name="B01")
         B2 = const.tile([P, H], F32, name="B2")
         bU2 = const.tile([P, H], F32, name="bU2")
 
-        def spread(vec, c, j, tag="acc"):
+        def spread(c, tag="acc"):
             ps = psum.tile([P, NB], F32, name="ps", tag=tag, bufs=6 if tag == "acc" else 2)
-            k = j % 3
-            nc.tensor.matmul(out=ps[:], lhsT=coef[:, c:c + 1].to_broadcast([P, P]),
-                             rhs=vec[:, k * NB:(k + 1) * NB], start=True, stop=True)
+            nc.tensor.matmul(out=ps[:], lhsT=coef[:, c:c + 1].to_broadcast([P, P]), rhs=bvec[:], start=True, stop=True)
             return ps
 
-        def spread_gamma(w):
-            for j in range(BANKS):
-                ps = spread(gvec[w], j // 3, j, "acc" if w == 0 else "aux")
-                if w == 0 and j % 2:
-                    nc.vector.tensor_copy(out=gam[w][:, j * NB:(j + 1) * NB], in_=ps[:])
-                else:
-                    nc.scalar.copy(out=gam[w][:, j * NB:(j + 1) * NB], in_=ps[:])
+        def warm_up():
+            for j in range(WARM):
+                ps = psum.tile([P, NB], F32, name="wu", tag="aux", bufs=2)
+                nc.tensor.matmul(out=ps[:], lhsT=cold[:, 0:P], rhs=cold[:], start=True, stop=True)
+
+        def gamma_pair(w, j0, tag):
+            ps = psum.tile([P, H], BF16, name="gs", tag=tag, bufs=6 if tag == "acc" else 2)
+            for k, (lo, hi) in enumerate(HALVES):
+                c = 3 * BANKS * w + j0 + k
+                nc.tensor.matmul(out=ps[:, lo:hi], lhsT=coef[:, c:c + 1].to_broadcast([P, P]),
+                                 rhs=(bvec if w else gvec)[:], start=True, stop=True)
+            nc.scalar.copy(out=gam[w][:, j0 * NB:(j0 + 2) * NB], in_=ps[:])
 
         def table(j):
-            ps = spread(bvec, 4 if j > 3 else 2 + j // 3, j, "aux")
+            ps = spread(4 * BANKS + j, "aux")
             dst = B2[:, (j - 4) * NB:(j - 3) * NB] if j > 3 else B01[:, j * NB:(j + 1) * NB]
             nc.scalar.copy(out=dst, in_=ps[:])
 
@@ -154,11 +157,12 @@ def tile_lngrucell_kernel(tc, x_in, hx, W_words, W_scales, U_words, U_scales,
             scls[(i, w)] = sc
 
         def mx(dst, i, w, j, g, start, stop):
+            tile, first = [(t, c[0]) for t, c in zip(words[w], chunks[w]) if c[0] <= j < c[1]][0]
             nc.tensor.matmul_mx(
                 out=dst[:],
                 lhsT=codes[(i, w)][:, g * P:(g + 1) * P].bitcast(FP8X4),
                 lhsT_scale=scls[(i, w)][:, g * P:(g + 1) * P],
-                rhs=words[w][:, g, 2 * NB * j:2 * NB * (j + 1)].bitcast(FP4X4),
+                rhs=tile[:, g, 2 * NB * (j - first):2 * NB * (j - first + 1)].bitcast(FP4X4),
                 rhs_scale=planes[w][:, g, NB * j:NB * (j + 1)],
                 start=start, stop=stop,
             )
@@ -195,11 +199,10 @@ def tile_lngrucell_kernel(tc, x_in, hx, W_words, W_scales, U_words, U_scales,
             nc.vector.scalar_tensor_tensor(out=dst[:, j * NB:(j + 1) * NB], in0=acc[:], scalar=mus[(i, w)][:, 0:1],
                                            in1=gam[w][:, j * NB:(j + 1) * NB], op0=ALU.subtract, op1=ALU.mult)
 
-        def unit_bank(i, w, j, acc=None):
+        def unit_bank(i, w, j):
             if j == 0:
                 s2s[(i, w)] = small.tile([P, BANKS], F32, name="s2", tag="s2")
-            if acc is None:
-                acc = product(i, w, j)
+            acc = product(i, w, j)
             scale_gamma(i, w, j, acc)
             junk = small.tile([P, NB], BF16, name="junk", tag="junk")
             nc.scalar.activation(out=junk[:], in_=acc[:], func=ACT.Square, scale=-1.0, bias=mus[(i, w)][:, 0:1],
@@ -261,26 +264,22 @@ def tile_lngrucell_kernel(tc, x_in, hx, W_words, W_scales, U_words, U_scales,
             nc.vector.scalar_tensor_tensor(out=t, in0=t, scalar=rss[(i, 1)][:, 0:1], in1=bU2[:],
                                            op0=ALU.mult, op1=ALU.add)
 
-        def scale_ps(i, part):
+        def scale_ps(i, part, tag="acc"):
             banks = []
             for k, (lo, hi) in enumerate(HALVES):
                 j = 2 * part + k
-                ps = spread(bvec, 4 if part == 2 else 2 + j // 3, j)
+                ps = spread(4 * BANKS + j, tag)
                 u = us[i][:, cols(part, lo, hi)]
                 nc.vector.scalar_tensor_tensor(out=u, in0=u, scalar=rss[(i, 0)][:, 0:1], in1=ps[:],
                                                op0=ALU.mult, op1=ALU.add)
                 banks.append(ps)
             return banks
 
-        def hu2_ps(i):
-            banks = []
-            for k, (lo, hi) in enumerate(HALVES):
-                ps = spread(bvec, 1, 4 + k)
+        def hu2_ps(i, banks):
+            for ps, (lo, hi) in zip(banks, HALVES):
                 t = ws[i][:, cols(2, lo, hi)]
                 nc.vector.scalar_tensor_tensor(out=t, in0=t, scalar=rss[(i, 1)][:, 0:1], in1=ps[:],
                                                op0=ALU.mult, op1=ALU.add)
-                banks.append(ps)
-            return banks
 
         def keep(banks, dst):
             for ps, (lo, hi) in zip(banks, HALVES):
@@ -290,6 +289,22 @@ def tile_lngrucell_kernel(tc, x_in, hx, W_words, W_scales, U_words, U_scales,
             u = us[i][:, cols(part)]
             nc.vector.scalar_tensor_tensor(out=u, in0=ws[i][:, cols(part)], scalar=rss[(i, 1)][:, 0:1], in1=u,
                                            op0=ALU.mult, op1=ALU.add)
+
+        def scale_pe(i, part):
+            banks = []
+            for k, (lo, hi) in enumerate(HALVES):
+                j = 2 * part + k
+                ps = psum.tile([P, NB], F32, name="ps", tag="acc", bufs=6)
+                c = 4 * BANKS + j
+                nc.tensor.matmul(out=ps[:], lhsT=coef[:, c:c + 1].to_broadcast([P, P]), rhs=bvec[:], start=True, stop=False)
+                nc.tensor.matmul(out=ps[:], lhsT=diag[:], rhs=us[i][:, cols(part, lo, hi)], start=False, stop=True)
+                banks.append(ps)
+            return banks
+
+        def add_pe(i, part, banks):
+            for ps, (lo, hi) in zip(banks, HALVES):
+                nc.vector.scalar_tensor_tensor(out=us[i][:, cols(part, lo, hi)], in0=ws[i][:, cols(part, lo, hi)],
+                                               scalar=rss[(i, 1)][:, 0:1], in1=ps[:], op0=ALU.mult, op1=ALU.add)
 
         def gate(i, part, lo=0, hi=H):
             u = us[i][:, cols(part, lo, hi)]
@@ -336,61 +351,65 @@ def tile_lngrucell_kernel(tc, x_in, hx, W_words, W_scales, U_words, U_scales,
             us[i] = work.tile([P, N3], F32, name="u", tag="u")
             ws[i] = work.tile([P, N3], F32, name="wt", tag="wt")
             if i == 0:
+                warm_up()
                 prep_t(0, 0)
                 prep_q(0, 0)
-                spread_gamma(0)
-                prep_t(0, 1)
-                prep_q(0, 1)
-                accs = first_stats(0, {
-                    3: (lambda: prep_t(1, 0), lambda: table(0)), 4: (lambda: table(1),),
-                    5: (lambda: prep_q(1, 0), lambda: table(2), lambda: table(3))})
+                for j in range(0, BANKS, 2):
+                    gamma_pair(0, j, "acc")
+                accs = first_stats(0, {5: (lambda: prep_t(0, 1), lambda: prep_t(1, 0), lambda: table(0), lambda: table(1))})
                 for j in range(BANKS):
                     scale_gamma(0, 0, j, accs[j])
-                table(4)
-                table(5)
+                    if j < 2:
+                        prep_q(j, 1 - j)
                 scale_g(0)
-                scale_s(1)
-                scale_s(2)
                 bias_g(0, B01[:, cols(0)])
-                bias_g(1, B01[:, cols(1)])
-                accs = first_stats(1, {})
-                bias_g(2, B2)
+                accs = first_stats(1, {0: (lambda: table(2),), 1: (lambda: table(3), lambda: scale_s(1), lambda: bias_g(1, B01[:, cols(1)])), 2: (lambda: table(4),),
+                                       3: (lambda: table(5), lambda: scale_s(2))})
                 prep_t(1, 1)
+                for j in range(0, BANKS, 2):
+                    gamma_pair(1, j, "aux")
                 for j in range(BANKS):
                     scale_gamma(0, 1, j, accs[j])
                 fold(1, 0)
                 mean(1, 0)
+                banks = [spread(4 + k) for k in range(2)]
                 prep_q(1, 1)
+                fold(1, 1)
+                bias_g(2, B2)
                 add_c(0, 1)
                 gate(0, 1)
                 add_c(0, 0)
                 gate(0, 0)
-                keep(hu2_ps(0), bU2)
+                hu2_ps(0, banks)
+                mean(1, 1)
+                keep(banks, bU2)
             else:
                 for lo, hi in HALVES:
                     cand_mul(nc.gpsimd, i - 1, lo, hi)
                 for lo, hi in HALVES:
                     cand_add(nc.gpsimd, i - 1, lo, hi)
-                early = []
-                if i == 1:
-                    early = [product(1, 0, j) for j in range(4)]
-                    fold(1, 1)
-                    mean(1, 1)
                 for j in range(BANKS):
-                    unit_bank(i, 0, j, early[j] if j < len(early) else None)
-                    if j >= BANKS - 2:
+                    unit_bank(i, 0, j)
+                    if j >= BANKS - 2 and i + 1 < BT:
                         lo, hi = HALVES[j - BANKS + 2]
                         gate(i - 1, 2, lo, hi)
                         blend_d(nc.gpsimd, i - 1, lo, hi)
                 unit_end(i, 0)
+                if i + 1 == BT:
+                    nc.gpsimd.tensor_scalar(out=diag[:], in0=ident[:], scalar1=rss[(i, 0)][:, 0:1], scalar2=0.0,
+                                            op0=ALU.mult, op1=ALU.add)
+                if i + 1 == BT:
+                    for lo, hi in HALVES:
+                        gate(i - 1, 2, lo, hi)
+                        blend_d(nc.gpsimd, i - 1, lo, hi)
                 if i + 1 < BT:
                     prep_t(i + 1, 0)
                     prep_t(i + 1, 1)
                 for j in range(BANKS):
                     unit_bank(i, 1, j)
                 if i + 1 == BT:
-                    for lo, hi in HALVES:
-                        blend_e(nc.gpsimd, i - 1, lo, hi)
+                    scale_ps(i, 2, "aux")
+                    blend_e(nc.vector, i - 1)
                 unit_end(i, 1)
                 if i + 1 < BT:
                     prep_q(i + 1, 0)
@@ -405,20 +424,20 @@ def tile_lngrucell_kernel(tc, x_in, hx, W_words, W_scales, U_words, U_scales,
                     blend_o(nc.vector, i - 1)
                     add_c(i, 1)
                     gate(i, 1)
-                    mean(i + 1, 1)
                     add_c(i, 0)
                     gate(i, 0)
+                    mean(i + 1, 1)
                     hu2(i)
         last = BT - 1
         for lo, hi in HALVES:
             blend_o(nc.gpsimd, last - 1, lo, hi)
-        scale_ps(last, 1)
-        scale_ps(last, 2)
-        scale_ps(last, 0)
-        hu2_ps(last)
-        add_c(last, 1)
-        gate(last, 1)
-        add_c(last, 0)
+        r_banks = scale_pe(last, 1)
+        hu2_ps(last, [spread(4 + k) for k in range(2)])
+        z_banks = scale_pe(last, 0)
+        add_pe(last, 1, r_banks)
+        for lo, hi in HALVES:
+            gate(last, 1, lo, hi)
+        add_pe(last, 0, z_banks)
         gate(last, 0)
         for lo, hi in HALVES:
             cand_mul(nc.vector, last, lo, hi)

@@ -23,7 +23,6 @@ BANKS = N3 // NB
 G = H // 512
 BT = B // P
 EPS = 1e-5
-WARM = 5
 FLOPS = 2 * 2 * B * H * N3
 HALVES = ((0, NB), (NB, H))
 
@@ -40,11 +39,11 @@ def tile_lngrucell_kernel(tc, x_in, hx, W_words, W_scales, U_words, U_scales,
         ctx.enter_context(tc.manual_schedule())
 
         planes = [const.tile([P, G, N3], U8, name="plane%d" % w, align_bytes=64) for w in range(2)]
-        chunks = (((0,2),(2,6)), ((0,3),(3,6)))
+        chunks = (((0,2),(2,4),(4,6)), ((0,3),(3,6)))
         words = [[const.tile([P, G, 2 * NB * (last - first)], U8, name="words%d_%d" % (w, first), align_bytes=64)
                   for first, last in chunks[w]] for w in range(2)]
         gvec = const.tile([P, NB], BF16, name="gvec")
-        gam = [const.tile([P, N3], BF16, name="gam%d" % w) for w in range(2)]
+        gam = [const.tile([P, N3], F32 if w == 0 else BF16, name="gam%d" % w) for w in range(2)]
         bvec = const.tile([P, NB], BF16, name="bvec")
         mhalf = const.tile([P, 1], F32, name="mhalf")
         warm = const.tile([P, 1], F32, name="warm")
@@ -73,11 +72,12 @@ def tile_lngrucell_kernel(tc, x_in, hx, W_words, W_scales, U_words, U_scales,
             nc.sync.dma_start(out=dst[i][:], in_=src[i * P:(i + 1) * P, :])
 
         def load_scales(w, src, first, last):
-            for r in range(first, last):
-                nc.sync.dma_start(
-                    out=planes[w][r:P:32, :, :].bitcast(I32),
-                    in_=src[:, r:16:4, :].rearrange("g q n -> q g n").bitcast(I32),
-                )
+            for half in range(2):
+                for r in range(first, last):
+                    nc.sync.dma_start(
+                        out=planes[w][32 * half + r:P:64, :, :].bitcast(I32),
+                        in_=src[:, 4 * half + r:16:8, :].rearrange("g q n -> q g n").bitcast(I32),
+                    )
 
         def load_words(w, src):
             for tile, (first, last) in zip(words[w], chunks[w]):
@@ -95,9 +95,9 @@ def tile_lngrucell_kernel(tc, x_in, hx, W_words, W_scales, U_words, U_scales,
         load_rows(x_sb, x_in, 0)
         load_scales(0, W_scales, 0, 4)
         load_words(0, W_words)
-        load_scales(1, U_scales, 0, 4)
         load_rows(h_sb, hx, 0)
         load_rows(x_sb, x_in, 1)
+        load_scales(1, U_scales, 0, 4)
         load_words(1, U_words)
         load_rows(h_sb, hx, 1)
         for i in range(2, BT):
@@ -113,8 +113,8 @@ def tile_lngrucell_kernel(tc, x_in, hx, W_words, W_scales, U_words, U_scales,
             nc.tensor.matmul(out=ps[:], lhsT=coef[:, c:c + 1].to_broadcast([P, P]), rhs=bvec[:], start=True, stop=True)
             return ps
 
-        def warm_up():
-            for j in range(WARM):
+        def warm_up(passes):
+            for j in range(passes):
                 ps = psum.tile([P, NB], F32, name="wu", tag="aux", bufs=2)
                 nc.tensor.matmul(out=ps[:], lhsT=cold[:, 0:P], rhs=cold[:], start=True, stop=True)
 
@@ -351,17 +351,18 @@ def tile_lngrucell_kernel(tc, x_in, hx, W_words, W_scales, U_words, U_scales,
             us[i] = work.tile([P, N3], F32, name="u", tag="u")
             ws[i] = work.tile([P, N3], F32, name="wt", tag="wt")
             if i == 0:
-                warm_up()
+                warm_up(3)
                 prep_t(0, 0)
                 prep_q(0, 0)
                 for j in range(0, BANKS, 2):
                     gamma_pair(0, j, "acc")
+                warm_up(2)
                 accs = first_stats(0, {5: (lambda: prep_t(0, 1), lambda: prep_t(1, 0), lambda: table(0), lambda: table(1))})
                 for j in range(BANKS):
                     scale_gamma(0, 0, j, accs[j])
                     if j < 2:
                         prep_q(j, 1 - j)
-                scale_g(0)
+                scale_s(0)
                 bias_g(0, B01[:, cols(0)])
                 accs = first_stats(1, {0: (lambda: table(2),), 1: (lambda: table(3), lambda: scale_s(1), lambda: bias_g(1, B01[:, cols(1)])), 2: (lambda: table(4),),
                                        3: (lambda: table(5), lambda: scale_s(2))})

from contextlib import ExitStack

import concourse.mybir as mybir
from concourse.masks import make_identity

F32 = mybir.dt.float32
BF16 = mybir.dt.bfloat16
U8 = mybir.dt.uint8
U32 = mybir.dt.uint32
I32 = mybir.dt.int32
FP8X4 = mybir.dt.float8_e4m3fn_x4
FP4X4 = mybir.dt.float4_e2m1fn_x4
ALU = mybir.AluOpType
ACT = mybir.ActivationFunctionType
AX = mybir.AxisListType

P = 128
B = 512
H = 1024
N3 = 3 * H
NB = 512
BANKS = N3 // NB
G = H // 512
BT = B // P
EPS = 1e-5
FLOPS = 2 * 2 * B * H * N3
HALVES = ((0, NB), (NB, H))


def tile_lngrucell_kernel(tc, x_in, hx, W_words, W_scales, U_words, U_scales,
                                      b, W_gamma, W_beta, U_gamma, U_beta, out):
    nc = tc.nc
    with ExitStack() as ctx:
        const = ctx.enter_context(tc.tile_pool(name="const", bufs=1))
        xin = ctx.enter_context(tc.tile_pool(name="xin", bufs=4))
        work = ctx.enter_context(tc.tile_pool(name="work", bufs=3))
        small = ctx.enter_context(tc.tile_pool(name="small", bufs=4))
        psum = ctx.enter_context(tc.psum_pool(name="psum", bufs=1))
        ctx.enter_context(tc.manual_schedule())

        planes = [const.tile([P, G, N3], U8, name="plane%d" % w, align_bytes=64) for w in range(2)]
        chunks = (((0,2),(2,4),(4,6)), ((0,3),(3,6)))
        words = [[const.tile([P, G, 2 * NB * (last - first)], U8, name="words%d_%d" % (w, first), align_bytes=64)
                  for first, last in chunks[w]] for w in range(2)]
        gvec = const.tile([P, NB], BF16, name="gvec")
        gam = [const.tile([P, N3], F32 if w == 0 else BF16, name="gam%d" % w) for w in range(2)]
        bvec = const.tile([P, NB], BF16, name="bvec")
        mhalf = const.tile([P, 1], F32, name="mhalf")
        warm = const.tile([P, 1], F32, name="warm")
        ident = const.tile([P, P], F32, name="ident")
        cold = const.tile([P, NB], BF16, name="cold")
        diag = const.tile([P, P], F32, name="diag")
        x_sb = [const.tile([P, H], BF16, name="x_sb%d" % i) for i in range(BT)]
        h_sb = [const.tile([P, H], BF16, name="h_sb%d" % i) for i in range(BT)]

        nc.vector.memset(cold[:].bitcast(I32), 0)
        nc.vector.memset(gvec[:].bitcast(I32), 0)
        nc.vector.memset(planes[0][:].rearrange("p g n -> p (g n)").bitcast(I32), 0)
        nc.vector.memset(bvec[:].bitcast(I32), 0)
        nc.vector.memset(mhalf[:], -0.5)
        make_identity(nc, ident[:])

        coef32 = const.tile([P, BANKS], F32, name="coef32")
        coef = const.tile([P, 5 * BANKS], BF16, name="coef")
        nc.vector.tensor_copy(out=coef[:, 0:4 * BANKS], in_=ident[:, 0:4 * BANKS])
        nc.vector.tensor_tensor(out=coef32[:], in0=ident[:, BANKS:2 * BANKS], in1=ident[:, 2 * BANKS:3 * BANKS], op=ALU.add)
        nc.vector.memset(planes[1][:].rearrange("p g n -> p (g n)").bitcast(I32), 0)
        nc.vector.tensor_tensor(out=coef[:, 4 * BANKS:4 * BANKS + 4], in0=coef32[:, 0:4], in1=ident[:, 0:4], op=ALU.add)
        nc.vector.tensor_copy(out=coef[:, 4 * BANKS + 4:5 * BANKS], in_=coef32[:, 4:BANKS])

        def load_rows(dst, src, i):
            nc.sync.dma_start(out=dst[i][:], in_=src[i * P:(i + 1) * P, :])

        def load_scales(w, src, first, last):
            for half in range(2):
                for r in range(first, last):
                    nc.sync.dma_start(
                        out=planes[w][32 * half + r:P:64, :, :].bitcast(I32),
                        in_=src[:, 4 * half + r:16:8, :].rearrange("g q n -> q g n").bitcast(I32),
                    )

        def load_words(w, src):
            for tile, (first, last) in zip(words[w], chunks[w]):
                nc.sync.dma_start(
                    out=tile[:].bitcast(I32),
                    in_=src[:, :, 2 * NB * first:2 * NB * last].rearrange("g p c -> p g c").bitcast(I32))

        def load_vec(dst, v, src):
            nc.gpsimd.dma_start(out=dst[BANKS * v:BANKS * (v + 1), :], in_=src.rearrange("(j n) -> j n", n=NB))

        nc.scalar.activation(out=warm[:], in_=mhalf[:], func=ACT.Sigmoid)
        load_vec(gvec, 0, W_gamma)
        for v, src in enumerate((U_beta, W_beta, b, U_gamma)):
            load_vec(bvec, v, src)
        load_rows(x_sb, x_in, 0)
        load_scales(0, W_scales, 0, 4)
        load_words(0, W_words)
        load_rows(h_sb, hx, 0)
        load_rows(x_sb, x_in, 1)
        load_scales(1, U_scales, 0, 4)
        load_words(1, U_words)
        load_rows(h_sb, hx, 1)
        for i in range(2, BT):
            load_rows(x_sb, x_in, i)
            load_rows(h_sb, hx, i)

        B01 = const.tile([P, 2 * H], F32, name="B01")
        B2 = const.tile([P, H], F32, name="B2")
        bU2 = const.tile([P, H], F32, name="bU2")

        def spread(c, tag="acc"):
            ps = psum.tile([P, NB], F32, name="ps", tag=tag, bufs=6 if tag == "acc" else 2)
            nc.tensor.matmul(out=ps[:], lhsT=coef[:, c:c + 1].to_broadcast([P, P]), rhs=bvec[:], start=True, stop=True)
            return ps

        def warm_up(passes):
            for j in range(passes):
                ps = psum.tile([P, NB], F32, name="wu", tag="aux", bufs=2)
                nc.tensor.matmul(out=ps[:], lhsT=cold[:, 0:P], rhs=cold[:], start=True, stop=True)

        def gamma_pair(w, j0, tag):
            ps = psum.tile([P, H], BF16, name="gs", tag=tag, bufs=6 if tag == "acc" else 2)
            for k, (lo, hi) in enumerate(HALVES):
                c = 3 * BANKS * w + j0 + k
                nc.tensor.matmul(out=ps[:, lo:hi], lhsT=coef[:, c:c + 1].to_broadcast([P, P]),
                                 rhs=(bvec if w else gvec)[:], start=True, stop=True)
            nc.scalar.copy(out=gam[w][:, j0 * NB:(j0 + 2) * NB], in_=ps[:])

        def table(j):
            ps = spread(4 * BANKS + j, "aux")
            dst = B2[:, (j - 4) * NB:(j - 3) * NB] if j > 3 else B01[:, j * NB:(j + 1) * NB]
            nc.scalar.copy(out=dst, in_=ps[:])

        codes = {}
        scls = {}
        groups = {}

        def prep_t(i, w):
            src32 = (x_sb[i] if w == 0 else h_sb[i])[:].bitcast(F32)
            xt = psum.tile([P, NB], F32, name="xt", tag="aux", bufs=2)
            for g in range(G):
                for u in range(2):
                    nc.tensor.transpose(xt[:, (2 * g + u) * P:(2 * g + u + 1) * P],
                                        src32[:, 256 * g + u:256 * (g + 1):2], ident[:])
            grouped = xin.tile([P, NB], F32, name="grouped", tag="grouped", align_bytes=64)
            nc.scalar.copy(
                out=grouped[:].rearrange("p (g b u) -> p g b u", g=G, u=2),
                in_=xt[:].rearrange("p (g u b) -> p g b u", g=G, u=2),
            )
            groups[(i, w)] = grouped

        def prep_q(i, w):
            cd = const.tile([P, G * P], U32, name="codes%d_%d" % (w, i), align_bytes=64)
            sc = const.tile([P, G * P], U8, name="scl%d_%d" % (w, i), align_bytes=64)
            nc.vector.quantize_mx(out=cd[:].bitcast(FP8X4), scales=sc[:], in_=groups[(i, w)][:].bitcast(BF16))
            codes[(i, w)] = cd
            scls[(i, w)] = sc

        def mx(dst, i, w, j, g, start, stop):
            tile, first = [(t, c[0]) for t, c in zip(words[w], chunks[w]) if c[0] <= j < c[1]][0]
            nc.tensor.matmul_mx(
                out=dst[:],
                lhsT=codes[(i, w)][:, g * P:(g + 1) * P].bitcast(FP8X4),
                lhsT_scale=scls[(i, w)][:, g * P:(g + 1) * P],
                rhs=tile[:, g, 2 * NB * (j - first):2 * NB * (j - first + 1)].bitcast(FP4X4),
                rhs_scale=planes[w][:, g, NB * j:NB * (j + 1)],
                start=start, stop=stop,
            )

        def product(i, w, j):
            acc = psum.tile([P, NB], F32, name="acc", tag="acc", bufs=6)
            for g in range(G):
                mx(acc, i, w, j, g, g == 0, g == G - 1)
            return acc

        folds = {}
        mus = {}
        s2s = {}
        rss = {}
        us = {}
        ws = {}

        def fold(i, w):
            f = psum.tile([P, NB], F32, name="fold", tag="aux", bufs=2)
            for j in range(BANKS):
                for g in range(G):
                    mx(f, i, w, j, g, j == 0 and g == 0, j == BANKS - 1 and g == G - 1)
            folds[(i, w)] = f

        def mean(i, w):
            mu = small.tile([P, 1], F32, name="mu", tag="mu")
            junk = small.tile([P, NB], BF16, name="junk", tag="junk")
            nc.scalar.activation(out=junk[:], in_=folds[(i, w)][:], func=ACT.Identity, scale=1.0 / N3,
                                 accum_out=mu[:])
            mus[(i, w)] = mu

        def scale_gamma(i, w, j, acc):
            dst = us[i] if w == 0 else ws[i]
            nc.vector.scalar_tensor_tensor(out=dst[:, j * NB:(j + 1) * NB], in0=acc[:], scalar=mus[(i, w)][:, 0:1],
                                           in1=gam[w][:, j * NB:(j + 1) * NB], op0=ALU.subtract, op1=ALU.mult)

        def unit_bank(i, w, j):
            if j == 0:
                s2s[(i, w)] = small.tile([P, BANKS], F32, name="s2", tag="s2")
            acc = product(i, w, j)
            scale_gamma(i, w, j, acc)
            junk = small.tile([P, NB], BF16, name="junk", tag="junk")
            nc.scalar.activation(out=junk[:], in_=acc[:], func=ACT.Square, scale=-1.0, bias=mus[(i, w)][:, 0:1],
                                 accum_out=s2s[(i, w)][:, j:j + 1])

        def rstd(i, w, vs):
            rs = small.tile([P, 1], F32, name="rs", tag="rs")
            nc.gpsimd.tensor_tensor(out=rs[:], in0=vs[:], in1=mhalf[:], op=ALU.pow)
            rss[(i, w)] = rs

        def unit_end(i, w):
            vs = small.tile([P, 1], F32, name="vs", tag="vs")
            j6 = small.tile([P, BANKS], F32, name="j6", tag="j6")
            nc.scalar.activation(out=j6[:], in_=s2s[(i, w)][:], func=ACT.Identity, scale=1.0 / N3, bias=EPS / BANKS,
                                 accum_out=vs[:])
            rstd(i, w, vs)

        def first_stats(w, beside):
            stats = small.tile([P, BANKS, 6], F32, name="stats", tag="stats")
            mv = small.tile([P, 2], F32, name="mv", tag="mv")
            vs = small.tile([P, 1], F32, name="vs", tag="vs")
            accs = []
            for j in range(BANKS):
                acc = product(0, w, j)
                nc.vector.bn_stats(out=stats[:, j, :], in_=acc[:])
                accs.append(acc)
                for f in beside.get(j, ()):
                    f()
            nc.vector.bn_aggr(out=mv[:], in_=stats[:].rearrange("p j s -> p (j s)"))
            mus[(0, w)] = mv
            nc.gpsimd.tensor_scalar(out=vs[:], in0=mv[:, 1:2], scalar1=EPS, scalar2=None, op0=ALU.add)
            rstd(0, w, vs)
            return accs

        def cols(part, lo=0, hi=H):
            return slice(part * H + lo, part * H + hi)

        def scale_a(i, part):
            bias = B2[:] if part == 2 else B01[:, cols(part)]
            u = us[i][:, cols(part)]
            nc.vector.scalar_tensor_tensor(out=u, in0=u, scalar=rss[(i, 0)][:, 0:1], in1=bias,
                                           op0=ALU.mult, op1=ALU.add)

        def scale_g(part):
            u = us[0][:, cols(part)]
            nc.gpsimd.tensor_scalar(out=u, in0=u, scalar1=rss[(0, 0)][:, 0:1], scalar2=0.0, op0=ALU.mult, op1=ALU.add)

        def scale_s(part):
            u = us[0][:, cols(part)]
            nc.scalar.activation(out=u, in_=u, func=ACT.Identity, scale=rss[(0, 0)][:, 0:1])

        def bias_g(part, bias):
            for lo, hi in HALVES:
                u = us[0][:, cols(part, lo, hi)]
                nc.gpsimd.tensor_tensor(out=u, in0=u, in1=bias[:, lo:hi], op=ALU.add)

        def hu2(i):
            t = ws[i][:, cols(2)]
            nc.vector.scalar_tensor_tensor(out=t, in0=t, scalar=rss[(i, 1)][:, 0:1], in1=bU2[:],
                                           op0=ALU.mult, op1=ALU.add)

        def scale_ps(i, part, tag="acc"):
            banks = []
            for k, (lo, hi) in enumerate(HALVES):
                j = 2 * part + k
                ps = spread(4 * BANKS + j, tag)
                u = us[i][:, cols(part, lo, hi)]
                nc.vector.scalar_tensor_tensor(out=u, in0=u, scalar=rss[(i, 0)][:, 0:1], in1=ps[:],
                                               op0=ALU.mult, op1=ALU.add)
                banks.append(ps)
            return banks

        def hu2_ps(i, banks):
            for ps, (lo, hi) in zip(banks, HALVES):
                t = ws[i][:, cols(2, lo, hi)]
                nc.vector.scalar_tensor_tensor(out=t, in0=t, scalar=rss[(i, 1)][:, 0:1], in1=ps[:],
                                               op0=ALU.mult, op1=ALU.add)

        def keep(banks, dst):
            for ps, (lo, hi) in zip(banks, HALVES):
                nc.scalar.copy(out=dst[:, lo:hi], in_=ps[:])

        def add_c(i, part):
            u = us[i][:, cols(part)]
            nc.vector.scalar_tensor_tensor(out=u, in0=ws[i][:, cols(part)], scalar=rss[(i, 1)][:, 0:1], in1=u,
                                           op0=ALU.mult, op1=ALU.add)

        def scale_pe(i, part):
            banks = []
            for k, (lo, hi) in enumerate(HALVES):
                j = 2 * part + k
                ps = psum.tile([P, NB], F32, name="ps", tag="acc", bufs=6)
                c = 4 * BANKS + j
                nc.tensor.matmul(out=ps[:], lhsT=coef[:, c:c + 1].to_broadcast([P, P]), rhs=bvec[:], start=True, stop=False)
                nc.tensor.matmul(out=ps[:], lhsT=diag[:], rhs=us[i][:, cols(part, lo, hi)], start=False, stop=True)
                banks.append(ps)
            return banks

        def add_pe(i, part, banks):
            for ps, (lo, hi) in zip(banks, HALVES):
                nc.vector.scalar_tensor_tensor(out=us[i][:, cols(part, lo, hi)], in0=ws[i][:, cols(part, lo, hi)],
                                               scalar=rss[(i, 1)][:, 0:1], in1=ps[:], op0=ALU.mult, op1=ALU.add)

        def gate(i, part, lo=0, hi=H):
            u = us[i][:, cols(part, lo, hi)]
            nc.scalar.activation(out=u, in_=u, func=ACT.Tanh if part == 2 else ACT.Sigmoid)

        def cand_mul(eng, i, lo, hi):
            t = ws[i][:, cols(2, lo, hi)]
            eng.tensor_tensor(out=t, in0=us[i][:, cols(1, lo, hi)], in1=t, op=ALU.mult)

        def cand_add(eng, i, lo, hi):
            n = us[i][:, cols(2, lo, hi)]
            eng.tensor_tensor(out=n, in0=ws[i][:, cols(2, lo, hi)], in1=n, op=ALU.add)

        def blend_d(eng, i, lo=0, hi=H):
            eng.tensor_tensor(out=ws[i][:, cols(2, lo, hi)], in0=h_sb[i][:, lo:hi], in1=us[i][:, cols(2, lo, hi)],
                              op=ALU.subtract)

        def blend_e(eng, i, lo=0, hi=H):
            t = ws[i][:, cols(2, lo, hi)]
            eng.tensor_tensor(out=t, in0=us[i][:, cols(0, lo, hi)], in1=t, op=ALU.mult)

        def store(i, lo, hi):
            nc.sync.dma_start(out=out[i * P:(i + 1) * P, lo:hi], in_=ws[i][:, cols(2, lo, hi)])

        def blend_o(eng, i, lo=0, hi=H):
            t = ws[i][:, cols(2, lo, hi)]
            eng.tensor_tensor(out=t, in0=t, in1=us[i][:, cols(2, lo, hi)], op=ALU.add)
            store(i, lo, hi)

        def blend_zh(i):
            nc.vector.tensor_tensor(out=ws[i][:, cols(0)], in0=us[i][:, cols(0)], in1=h_sb[i][:], op=ALU.mult)

        def blend_zn(i, lo, hi):
            t = ws[i][:, cols(2, lo, hi)]
            nc.vector.scalar_tensor_tensor(out=t, in0=us[i][:, cols(0, lo, hi)], scalar=1.0,
                                           in1=us[i][:, cols(2, lo, hi)], op0=ALU.subtract, op1=ALU.mult)

        def blend_s(i, lo, hi):
            t = ws[i][:, cols(2, lo, hi)]
            nc.vector.tensor_tensor(out=t, in0=ws[i][:, cols(0, lo, hi)], in1=t, op=ALU.subtract)
            store(i, lo, hi)

        for i in range(BT):
            us[i] = work.tile([P, N3], F32, name="u", tag="u")
            ws[i] = work.tile([P, N3], F32, name="wt", tag="wt")
            if i == 0:
                warm_up(3)
                prep_t(0, 0)
                prep_q(0, 0)
                for j in range(0, BANKS, 2):
                    gamma_pair(0, j, "acc")
                warm_up(2)
                accs = first_stats(0, {5: (lambda: prep_t(0, 1), lambda: prep_t(1, 0), lambda: table(0), lambda: table(1))})
                for j in range(BANKS):
                    scale_gamma(0, 0, j, accs[j])
                    if j < 2:
                        prep_q(j, 1 - j)
                scale_s(0)
                bias_g(0, B01[:, cols(0)])
                accs = first_stats(1, {0: (lambda: table(2),), 1: (lambda: table(3), lambda: scale_s(1), lambda: bias_g(1, B01[:, cols(1)])), 2: (lambda: table(4),),
                                       3: (lambda: table(5), lambda: scale_s(2))})
                prep_t(1, 1)
                for j in range(0, BANKS, 2):
                    gamma_pair(1, j, "aux")
                for j in range(BANKS):
                    scale_gamma(0, 1, j, accs[j])
                fold(1, 0)
                mean(1, 0)
                banks = [spread(4 + k) for k in range(2)]
                prep_q(1, 1)
                fold(1, 1)
                bias_g(2, B2)
                add_c(0, 1)
                gate(0, 1)
                add_c(0, 0)
                gate(0, 0)
                hu2_ps(0, banks)
                mean(1, 1)
                keep(banks, bU2)
            else:
                for lo, hi in HALVES:
                    cand_mul(nc.gpsimd, i - 1, lo, hi)
                for lo, hi in HALVES:
                    cand_add(nc.gpsimd, i - 1, lo, hi)
                for j in range(BANKS):
                    unit_bank(i, 0, j)
                    if j >= BANKS - 2 and i + 1 < BT:
                        lo, hi = HALVES[j - BANKS + 2]
                        gate(i - 1, 2, lo, hi)
                        blend_d(nc.gpsimd, i - 1, lo, hi)
                unit_end(i, 0)
                if i + 1 == BT:
                    nc.gpsimd.tensor_scalar(out=diag[:], in0=ident[:], scalar1=rss[(i, 0)][:, 0:1], scalar2=0.0,
                                            op0=ALU.mult, op1=ALU.add)
                if i + 1 == BT:
                    for lo, hi in HALVES:
                        gate(i - 1, 2, lo, hi)
                        blend_d(nc.gpsimd, i - 1, lo, hi)
                if i + 1 < BT:
                    prep_t(i + 1, 0)
                    prep_t(i + 1, 1)
                for j in range(BANKS):
                    unit_bank(i, 1, j)
                if i + 1 == BT:
                    scale_ps(i, 2, "aux")
                    blend_e(nc.vector, i - 1)
                unit_end(i, 1)
                if i + 1 < BT:
                    prep_q(i + 1, 0)
                    prep_q(i + 1, 1)
                    fold(i + 1, 0)
                    mean(i + 1, 0)
                    fold(i + 1, 1)
                    scale_a(i, 1)
                    scale_a(i, 0)
                    blend_e(nc.vector, i - 1)
                    scale_a(i, 2)
                    blend_o(nc.vector, i - 1)
                    add_c(i, 1)
                    gate(i, 1)
                    add_c(i, 0)
                    gate(i, 0)
                    mean(i + 1, 1)
                    hu2(i)
        last = BT - 1
        for lo, hi in HALVES:
            blend_o(nc.gpsimd, last - 1, lo, hi)
        r_banks = scale_pe(last, 1)
        hu2_ps(last, [spread(4 + k) for k in range(2)])
        z_banks = scale_pe(last, 0)
        add_pe(last, 1, r_banks)
        for lo, hi in HALVES:
            gate(last, 1, lo, hi)
        add_pe(last, 0, z_banks)
        gate(last, 0)
        for lo, hi in HALVES:
            cand_mul(nc.vector, last, lo, hi)
        for lo, hi in HALVES:
            cand_add(nc.vector, last, lo, hi)
            gate(last, 2, lo, hi)
        blend_zh(last)
        for lo, hi in HALVES:
            blend_zn(last, lo, hi)
        for lo, hi in HALVES:
            blend_s(last, lo, hi)
